import numpy as np
import ml_dtypes


def mxq(x, axis, fmt="e4m3"):
    dtype, down = {"e4m3": (ml_dtypes.float8_e4m3fn, 7), "e5m2": (ml_dtypes.float8_e5m2, 14)}[fmt]
    v = np.moveaxis(np.asarray(x, np.float32).astype(ml_dtypes.bfloat16).astype(np.float64), axis, -1)
    blocks = v.reshape(v.shape[:-1] + (-1, 32))
    amax = np.abs(blocks).max(-1, keepdims=True)
    byte = np.maximum(np.where(amax > 0, np.frexp(amax)[1] - 1 + 127, 0) - down, 1)
    scale = np.exp2(byte - 127.0)
    codes = (blocks / scale).astype(np.float32).astype(dtype).astype(np.float64)
    return np.moveaxis((codes * scale).reshape(v.shape), -1, axis)


WIDE = False


def mx_kscale(k):
    if not WIDE:
        return np.ones(k)
    levels = np.array([10, -10, 5, -5, 0])
    if k % 512:
        return np.exp2(np.random.permutation(np.resize(levels, k // 32))).repeat(32)
    a = np.empty((k // 512, 16))
    for p in range(k // 512):
        a[p, :8] = np.random.permutation(np.resize(levels, 8))
        for g in range(8):
            far = levels[np.abs(levels - a[p, g]) >= 10]
            a[p, g + 8] = far[np.random.randint(len(far))]
    return np.exp2(a.ravel()).repeat(32)


BF16 = ml_dtypes.bfloat16


def bf(x):
    return np.asarray(x, np.float32).astype(BF16)


def f64(x):
    return np.asarray(x).astype(np.float64)


B, S, D_MODEL, N_HEADS, QK_ROPE, QK_NOPE, KV_LORA, V_DIM = 2, 256, 2048, 16, 128, 128, 512, 128
RMS_EPS = 1.1920928955078125e-07
ROPE_BASE = 10000.0


def apply_rope(r):
    freqs = 1.0 / (ROPE_BASE ** (np.arange(0, QK_ROPE, 2) / QK_ROPE))
    t = np.arange(S)[:, None] * freqs[None, :]
    cos = np.cos(t)[None, :, None, :]
    sin = np.sin(t)[None, :, None, :]
    r1 = r[..., 0::2]
    r2 = r[..., 1::2]
    return np.stack([r1 * cos - r2 * sin, r2 * cos + r1 * sin], axis=-1).reshape(r.shape)


def setup_inputs():
    s, t = mx_kscale(D_MODEL), mx_kscale(KV_LORA)
    return {"x": bf(np.random.standard_normal((B, S, D_MODEL)) * s),
            "Wkv_a": bf(np.random.standard_normal((D_MODEL, KV_LORA + QK_ROPE)) / np.sqrt(D_MODEL) / s[:, None]),
            "kv_norm_w": bf((1.0 + 0.1 * np.random.standard_normal(KV_LORA)) * t),
            "Wkv_b": bf(np.random.standard_normal((KV_LORA, N_HEADS * (QK_NOPE + V_DIM))) / np.sqrt(KV_LORA) / t[:, None])}


def reference(x, Wkv_a, kv_norm_w, Wkv_b):
    kv = mxq(f64(x), 2, "e4m3") @ mxq(f64(Wkv_a), 0, "e4m3")
    c_kv, k_rope = kv[..., :KV_LORA], kv[..., KV_LORA:]
    k_rope = apply_rope(k_rope.reshape(B, S, 1, QK_ROPE))
    c_kv = c_kv * (1.0 / np.sqrt(np.mean(c_kv * c_kv, axis=-1, keepdims=True) + RMS_EPS)) * f64(kv_norm_w)
    kv = (mxq(c_kv, 2, "e4m3") @ mxq(f64(Wkv_b), 0, "e4m3")).reshape(B, S, N_HEADS, QK_NOPE + V_DIM)
    return kv[..., :QK_NOPE], kv[..., QK_NOPE:], k_rope

@@ -1,0 +1,399 @@
+from contextlib import ExitStack
+
+import concourse.mybir as mybir
+from concourse.masks import make_identity
+
+F32 = mybir.dt.float32
+BF16 = mybir.dt.bfloat16
+I32 = mybir.dt.int32
+U32 = mybir.dt.uint32
+U8 = mybir.dt.uint8
+FP8X4 = mybir.dt.float8_e4m3fn_x4
+ALU = mybir.AluOpType
+ACT = mybir.ActivationFunctionType
+
+P = 128
+PACK = 4
+K_PASS = P * PACK
+TOKENS = 512
+TILES = TOKENS // P
+SEQ_HALVES = 2
+D_MODEL = 2048
+PASSES = D_MODEL // K_PASS
+LATENT = 512
+ROPE = 128
+ROPE_PAIRS = ROPE // 2
+A_COLS = LATENT + ROPE
+KV_COLS = 4096
+HEAD_DIM = 128
+CHUNK_COLS = 1024
+CHUNK_HEADS = CHUNK_COLS // (2 * HEAD_DIM)
+CHUNKS = KV_COLS // CHUNK_COLS
+PIECE_COLS = CHUNK_HEADS * HEAD_DIM
+PIECES = 2 * CHUNKS
+RMS_EPS = 1.1920928955078125e-07
+ROPE_BASE = 10000.0
+TWO_PI = 6.283185307179586
+
+FLOPS = 2 * TOKENS * D_MODEL * A_COLS + 2 * TOKENS * LATENT * KV_COLS
+
+WA_VECTOR_COLS = 320
+RUN = 4
+
+
+def tile_multiheadlatentattention_pa_kernel(tc, x, Wkv_a, kv_norm_w, Wkv_b, out_0, out_1, out_2):
+    nc = tc.nc
+    x_rows = x.flatten_outer_dims()
+    kv_out = [
+        out_0.rearrange("b s h d -> (b s) (h d)"),
+        out_1.rearrange("b s h d -> (b s) (h d)"),
+    ]
+    with ExitStack() as ctx:
+        keep = ctx.enter_context(tc.tile_pool(name="keep", bufs=1))
+        regrouped = ctx.enter_context(tc.tile_pool(name="regrouped", bufs=3))
+        scrap = ctx.enter_context(tc.tile_pool(name="scrap", bufs=2))
+        leaving = ctx.enter_context(tc.tile_pool(name="leaving", bufs=12))
+        banks = ctx.enter_context(tc.psum_pool(name="banks", bufs=7))
+        rope_bank = ctx.enter_context(tc.psum_pool(name="rope_bank", bufs=1))
+        ctx.enter_context(tc.manual_schedule())
+
+        wa_raw = [keep.tile([P, PACK, A_COLS], BF16, name="wa_raw%d" % g) for g in range(PASSES)]
+        wa_grouped = [
+            keep.tile([P, A_COLS, PACK], BF16, name="wa_grouped%d" % g, align_bytes=64) for g in range(PASSES)
+        ]
+        wa_codes = keep.tile([P, PASSES, A_COLS], U32, name="wa_codes", align_bytes=64)
+        wa_scales = keep.tile([P, PASSES, A_COLS], U8, name="wa_scales", align_bytes=64)
+        x_raw = [keep.tile([P, D_MODEL], BF16, name="x_raw%d" % a) for a in range(TILES)]
+        x_grouped = [keep.tile([P, PASSES, P, 2], F32, name="x_grouped%d" % a, align_bytes=64) for a in range(TILES)]
+        x_codes = [keep.tile([P, PASSES * P], U32, name="x_codes%d" % a, align_bytes=64) for a in range(TILES)]
+        x_scales = [keep.tile([P, PASSES * P], U8, name="x_scales%d" % a, align_bytes=64) for a in range(TILES)]
+        sum_squares = [keep.tile([P, 1], F32, name="sum_squares%d" % a) for a in range(TILES)]
+        rms = [keep.tile([P, 1], F32, name="rms%d" % a) for a in range(TILES)]
+        inv_rms = [keep.tile([P, 1], F32, name="inv_rms%d" % a) for a in range(TILES)]
+        normed = [keep.tile([P, LATENT], BF16, name="normed%d" % a) for a in range(TILES)]
+        n_grouped = [keep.tile([P, P, PACK], BF16, name="n_grouped%d" % a, align_bytes=64) for a in range(TILES)]
+        n_codes = [keep.tile([P, P], U32, name="n_codes%d" % a, align_bytes=64) for a in range(TILES)]
+        n_scales = [keep.tile([P, P], U8, name="n_scales%d" % a, align_bytes=64) for a in range(TILES)]
+        wb_raw = [keep.tile([P, PACK, CHUNK_COLS], BF16, name="wb_raw%d" % c) for c in range(CHUNKS)]
+        wb_codes = keep.tile([P, PIECES, PIECE_COLS], U32, name="wb_codes", align_bytes=64)
+        wb_scales = keep.tile([P, PIECES, PIECE_COLS], U8, name="wb_scales", align_bytes=64)
+        raw_rope = rope_bank.tile([P, TILES, ROPE], F32, name="raw_rope")
+        in_psum = {}
+        wb_grouped = {}
+
+        eps = keep.tile([P, 1], F32, name="eps")
+        nc.vector.memset(eps[:], RMS_EPS)
+        table_loaded = keep.tile([P, 2], F32, name="table_loaded")
+        nc.scalar.activation(out=table_loaded[:, 0:1], in_=eps[:], func=ACT.Sin)
+        gain_row = keep.tile([P, LATENT], BF16, name="gain_row")
+        nc.vector.memset(gain_row[:], 0.0)
+        position_int = keep.tile([P, SEQ_HALVES], I32, name="position_int")
+        nc.gpsimd.iota(position_int[:], pattern=[[P, SEQ_HALVES]], base=0, channel_multiplier=1)
+
+        def load_wa(g):
+            nc.sync.dma_start(
+                out=wa_raw[g][:],
+                in_=Wkv_a[K_PASS * g : K_PASS * (g + 1), :].rearrange("(p t) c -> p t c", t=PACK),
+            )
+
+        def load_x(a):
+            nc.sync.dma_start(out=x_raw[a][:], in_=x_rows[P * a : P * (a + 1), :])
+
+        def load_wb(c):
+            nc.sync.dma_start(
+                out=wb_raw[c][:],
+                in_=Wkv_b[:, CHUNK_COLS * c : CHUNK_COLS * (c + 1)].rearrange("(p t) n -> p t n", t=PACK),
+            )
+
+        load_x(0)
+        load_x(1)
+        for g in range(PASSES):
+            load_wa(g)
+        nc.sync.dma_start(out=gain_row[0:1, :], in_=kv_norm_w.rearrange("(o n) -> o n", o=1))
+        load_x(2)
+        load_x(3)
+        for c in range(CHUNKS):
+            load_wb(c)
+
+        frequency = keep.tile([P, ROPE_PAIRS], F32, name="frequency")
+        nc.vector.memset(frequency[:, 0:1], 1.0)
+        for filled in (1, 2, 4, 8, 16, 32):
+            nc.vector.tensor_scalar_mul(
+                out=frequency[:, filled : 2 * filled],
+                in0=frequency[:, 0:filled],
+                scalar1=ROPE_BASE ** (-2.0 * filled / ROPE),
+            )
+        position = keep.tile([P, SEQ_HALVES], F32, name="position")
+        nc.vector.tensor_copy(out=position[:], in_=position_int[:])
+        turns = keep.tile([P, 2, SEQ_HALVES, ROPE_PAIRS], F32, name="turns")
+        for half in range(SEQ_HALVES):
+            nc.vector.tensor_scalar(
+                out=turns[:, 0, half, :],
+                in0=frequency[:],
+                scalar1=position[:, half : half + 1],
+                scalar2=1.0 / TWO_PI,
+                op0=ALU.mult,
+                op1=ALU.mult,
+            )
+        nc.vector.tensor_scalar_add(out=turns[:, 1, :, :], in0=turns[:, 0, :, :], scalar1=0.25)
+        turns_row = turns[:].rearrange("p s h i -> p (s h i)")
+        whole_int = keep.tile([P, 2 * P], I32, name="whole_int")
+        nc.vector.tensor_copy(out=whole_int[:], in_=turns_row)
+        whole = keep.tile([P, 2 * P], F32, name="whole")
+        nc.vector.tensor_copy(out=whole[:], in_=whole_int[:])
+        part_turn = keep.tile([P, 2 * P], F32, name="part_turn")
+        nc.vector.tensor_tensor(out=part_turn[:], in0=turns_row, in1=whole[:], op=ALU.subtract)
+        SIN, COS, MINUS_SIN = 0, 1, 2
+        trig = keep.tile([P, 3, SEQ_HALVES * ROPE_PAIRS], F32, name="trig")
+
+        ones = keep.tile([P, P], BF16, name="ones")
+        nc.vector.memset(ones[:], 1.0)
+        identity_f32 = keep.tile([P, P], F32, name="identity_f32")
+        make_identity(nc, identity_f32[:])
+        identity_bf16 = keep.tile([P, P], BF16, name="identity_bf16")
+        make_identity(nc, identity_bf16[:])
+        gain = keep.tile([P, LATENT], F32, name="gain")
+
+        def rope_tables_scalar():
+            nc.scalar.activation(
+                out=trig[:, SIN : COS + 1, :].rearrange("p s n -> p (s n)"), in_=part_turn[:], func=ACT.Sin, scale=TWO_PI
+            )
+            nc.scalar.activation(out=trig[:, MINUS_SIN, :], in_=part_turn[:, 0:P], func=ACT.Sin, scale=-TWO_PI)
+
+        def load_sqrt_table():
+            nc.scalar.activation(out=table_loaded[:, 1:2], in_=eps[:], func=ACT.Sqrt)
+
+        def regroup_wa(g):
+            for copy, first, last in (
+                (nc.scalar.copy, WA_VECTOR_COLS, A_COLS),
+                (nc.vector.tensor_copy, 0, WA_VECTOR_COLS),
+            ):
+                copy(
+                    out=wa_grouped[g][:, first:last, :].rearrange("p (c i) t -> p c t i", i=RUN),
+                    in_=wa_raw[g][:, :, first:last].rearrange("p t (c i) -> p c t i", i=RUN),
+                )
+
+        def quantise_wa(g, first, last):
+            nc.vector.quantize_mx(
+                out=wa_codes[:, g, first:last].bitcast(FP8X4),
+                scales=wa_scales[:, g, first:last],
+                in_=wa_grouped[g][:, first:last, :].rearrange("p c t -> p (c t)"),
+            )
+
+        def spread_gain():
+            summed = banks.tile([P, LATENT], F32, name="summed", tag="bank")
+            nc.tensor.matmul(out=summed[:], lhsT=ones[:], rhs=gain_row[:], start=True, stop=True)
+            nc.vector.tensor_copy(out=gain[:], in_=summed[:])
+
+        def transpose_x(a, copy):
+            words = x_raw[a][:].bitcast(F32)
+            for first_pass in range(0, PASSES, 2):
+                turned = banks.tile([P, 2, 2, P], F32, name="turned", tag="bank")
+                for g in range(2):
+                    for u in range(2):
+                        first_word = 2 * P * (first_pass + g)
+                        nc.tensor.transpose(
+                            turned[:, g, u, :], words[:, first_word + u : first_word + 2 * P : 2], identity_f32[:]
+                        )
+                copy(
+                    out=x_grouped[a][:, first_pass : first_pass + 2, :, :],
+                    in_=turned[:].rearrange("p g u r -> p g r u"),
+                )
+
+        def quantise_x(a):
+            for first_pass in range(0, PASSES, 2):
+                columns = slice(P * first_pass, P * (first_pass + 2))
+                nc.vector.quantize_mx(
+                    out=x_codes[a][:, columns].bitcast(FP8X4),
+                    scales=x_scales[a][:, columns],
+                    in_=x_grouped[a][:, first_pass : first_pass + 2, :, :].rearrange("p g r u -> p (g r u)").bitcast(BF16),
+                )
+
+        def first_matmul(a, out, first, last):
+            for g in range(PASSES):
+                nc.tensor.matmul_mx(
+                    out=out,
+                    lhsT=x_codes[a][:, P * g : P * (g + 1)].bitcast(FP8X4),
+                    lhsT_scale=x_scales[a][:, P * g : P * (g + 1)],
+                    rhs=wa_codes[:, g, first:last].bitcast(FP8X4),
+                    rhs_scale=wa_scales[:, g, first:last],
+                    start=(g == 0),
+                    stop=(g == PASSES - 1),
+                )
+
+        def latent(a):
+            in_psum["latent", a] = banks.tile([P, LATENT], F32, name="latent", tag="bank")
+            first_matmul(a, in_psum["latent", a][:], 0, LATENT)
+            squares = scrap.tile([P, LATENT], BF16, name="squares")
+            nc.scalar.activation(out=squares[:], in_=in_psum["latent", a][:], func=ACT.Square, accum_out=sum_squares[a][:])
+            nc.scalar.activation(out=rms[a][:], in_=sum_squares[a][:], func=ACT.Sqrt, scale=1.0 / LATENT, bias=eps[:])
+
+        def rope_key(a):
+            first_matmul(a, raw_rope[:, a, :], LATENT, A_COLS)
+
+        def normalise(a):
+            nc.vector.reciprocal(out=inv_rms[a][:], in_=rms[a][:])
+            nc.vector.scalar_tensor_tensor(
+                out=normed[a][:].rearrange("p (t q) -> p t q", t=PACK),
+                in0=in_psum["latent", a][:].rearrange("p (q t) -> p t q", t=PACK),
+                scalar=inv_rms[a][:],
+                in1=gain[:].rearrange("p (q t) -> p t q", t=PACK),
+                op0=ALU.mult,
+                op1=ALU.mult,
+            )
+
+        def transpose_n(a, copy):
+            turned = banks.tile([P, PACK, P], BF16, name="turned_n", tag="bank")
+            for t in range(PACK):
+                nc.tensor.transpose(turned[:, t, :], normed[a][:, P * t : P * (t + 1)], identity_bf16[:])
+            copy(out=n_grouped[a][:], in_=turned[:].rearrange("p t r -> p r t"))
+
+        def quantise_n(a):
+            nc.vector.quantize_mx(
+                out=n_codes[a][:].bitcast(FP8X4),
+                scales=n_scales[a][:],
+                in_=n_grouped[a][:].rearrange("p r t -> p (r t)"),
+            )
+
+        def regroup_wb(j):
+            wb_grouped[j] = regrouped.tile([P, PIECE_COLS, PACK], BF16, name="wb_grouped", align_bytes=64)
+            by_head = wb_raw[j // 2][:].rearrange(
+                "p t (h k c i) -> p t h k c i", h=CHUNK_HEADS, k=2, c=HEAD_DIM // RUN, i=RUN
+            )
+            nc.vector.tensor_copy(
+                out=wb_grouped[j][:].rearrange("p (h c i) t -> p h c t i", h=CHUNK_HEADS, c=HEAD_DIM // RUN, i=RUN),
+                in_=by_head[:, :, :, j % 2, :, :].rearrange("p t h c i -> p h c t i"),
+            )
+
+        def quantise_wb(j):
+            nc.vector.quantize_mx(
+                out=wb_codes[:, j, :].bitcast(FP8X4),
+                scales=wb_scales[:, j, :],
+                in_=wb_grouped[j][:].rearrange("p c t -> p (c t)"),
+            )
+
+        def second_matmul(a, j):
+            in_psum["kv", a, j] = banks.tile([P, PIECE_COLS], F32, name="kv", tag="bank")
+            nc.tensor.matmul_mx(
+                out=in_psum["kv", a, j][:],
+                lhsT=n_codes[a][:].bitcast(FP8X4),
+                lhsT_scale=n_scales[a][:],
+                rhs=wb_codes[:, j, :].bitcast(FP8X4),
+                rhs_scale=wb_scales[:, j, :],
+                start=True,
+                stop=True,
+            )
+
+        def store_kv(a, j):
+            out_tile = leaving.tile([P, PIECE_COLS], F32, name="out_tile")
+            if j == PIECES - 1 and a % 2 == 1:
+                nc.vector.tensor_copy(out=out_tile[:], in_=in_psum["kv", a, j][:])
+            else:
+                nc.scalar.copy(out=out_tile[:], in_=in_psum["kv", a, j][:])
+            nc.sync.dma_start(
+                out=kv_out[j % 2][P * a : P * (a + 1), PIECE_COLS * (j // 2) : PIECE_COLS * (j // 2 + 1)],
+                in_=out_tile[:],
+            )
+
+        def kv(products):
+            for a, j in products:
+                second_matmul(a, j)
+            for a, j in products:
+                store_kv(a, j)
+
+        pairs = raw_rope[:].rearrange("p (b h) (i e) -> p b (h i) e", b=2, e=2)
+        both = [P, 2, P]
+        by_cos = keep.tile([P, 2, P, 2], F32, name="by_cos")
+        by_sin = keep.tile([P, 2, 2, P], F32, name="by_sin")
+        k_rope = keep.tile([P, 2, P, 2], F32, name="k_rope")
+
+        def rope_by_cos():
+            nc.vector.tensor_tensor(
+                out=by_cos[:], in0=pairs, in1=trig[:, COS, :].unsqueeze(1).unsqueeze(3).to_broadcast([P, 2, P, 2]), op=ALU.mult
+            )
+
+        def rope_by_sin():
+            nc.vector.tensor_tensor(
+                out=by_sin[:, 0, :, :], in0=pairs[:, :, :, 1], in1=trig[:, MINUS_SIN, :].unsqueeze(1).to_broadcast(both), op=ALU.mult
+            )
+            nc.vector.tensor_tensor(
+                out=by_sin[:, 1, :, :], in0=pairs[:, :, :, 0], in1=trig[:, SIN, :].unsqueeze(1).to_broadcast(both), op=ALU.mult
+            )
+
+        def rope_sum():
+            nc.vector.tensor_tensor(
+                out=k_rope[:], in0=by_cos[:], in1=by_sin[:].rearrange("p e b n -> p b n e"), op=ALU.add
+            )
+            nc.sync.dma_start(
+                out=out_2.rearrange("b (h p) o d -> p (b h) (o d)", h=SEQ_HALVES, p=P),
+                in_=k_rope[:].rearrange("p b (h i) e -> p (b h) (i e)", h=SEQ_HALVES),
+            )
+
+        transpose_x(0, nc.scalar.copy)
+        transpose_x(1, nc.scalar.copy)
+        quantise_x(0)
+        regroup_wa(0)
+        quantise_x(1)
+        for g in range(PASSES):
+            if g + 1 < PASSES:
+                regroup_wa(g + 1)
+            if g == PASSES - 2:
+                spread_gain()
+            quantise_wa(g, 0, LATENT)
+        rope_tables_scalar()
+        load_sqrt_table()
+
+        transpose_x(2, nc.vector.tensor_copy)
+        transpose_x(3, nc.scalar.copy)
+        quantise_x(2)
+        regroup_wb(0)
+        quantise_x(3)
+
+        for a in range(TILES):
+            latent(a)
+        normalise(0)
+        quantise_wb(0)
+        normalise(1)
+        regroup_wb(1)
+        normalise(2)
+        quantise_wb(1)
+        for a in range(TILES - 1):
+            transpose_n(a, nc.scalar.copy)
+        quantise_n(0)
+        quantise_n(1)
+        regroup_wb(2)
+        quantise_n(2)
+        normalise(3)
+        quantise_wb(2)
+        regroup_wb(3)
+
+        early = ((0, 0), (1, 0), (0, 1), (1, 1), (2, 0), (2, 1))
+        for a, j in early:
+            second_matmul(a, j)
+        transpose_n(TILES - 1, nc.vector.tensor_copy)
+        quantise_n(TILES - 1)
+        for a, j in early:
+            store_kv(a, j)
+        quantise_wb(3)
+        regroup_wb(4)
+        quantise_wb(4)
+        kv(((0, 2), (1, 2), (2, 2)))
+        kv(((3, 0), (3, 1), (3, 2)))
+
+        for g in range(PASSES):
+            quantise_wa(g, LATENT, A_COLS)
+        for j in range(5, PIECES - 1):
+            regroup_wb(j)
+            quantise_wb(j)
+        regroup_wb(PIECES - 1)
+
+        for j in range(3, PIECES):
+            if j == 5:
+                for a in range(TILES):
+                    rope_key(a)
+            if j == PIECES - 1:
+                rope_by_cos()
+                rope_by_sin()
+                rope_sum()
+                quantise_wb(j)
+            kv([(a, j) for a in range(TILES)])

@@ -31,13 +31,16 @@ CHUNK_HEADS = CHUNK_COLS // (2 * HEAD_DIM)
 CHUNKS = KV_COLS // CHUNK_COLS
 PIECE_COLS = CHUNK_HEADS * HEAD_DIM
 PIECES = 2 * CHUNKS
+LOAD_COLS = (CHUNK_COLS, CHUNK_COLS, 2 * CHUNK_COLS)
+PIECE_ORDER = ((0, 0), (0, 1), (1, 0), (1, 1), (2, 0), (3, 0), (2, 1), (3, 1))
+FIRST_PAIRED = 4
 RMS_EPS = 1.1920928955078125e-07
 ROPE_BASE = 10000.0
 TWO_PI = 6.283185307179586
 
 FLOPS = 2 * TOKENS * D_MODEL * A_COLS + 2 * TOKENS * LATENT * KV_COLS
 
-WA_VECTOR_COLS = 320
+WA_VECTOR_COLS = 256
 RUN = 4
 
 
@@ -52,43 +55,36 @@ def tile_multiheadlatentattention_pa_kernel(tc, x, Wkv_a, kv_norm_w, Wkv_b, out_
         keep = ctx.enter_context(tc.tile_pool(name="keep", bufs=1))
         regrouped = ctx.enter_context(tc.tile_pool(name="regrouped", bufs=3))
         scrap = ctx.enter_context(tc.tile_pool(name="scrap", bufs=2))
-        leaving = ctx.enter_context(tc.tile_pool(name="leaving", bufs=12))
-        banks = ctx.enter_context(tc.psum_pool(name="banks", bufs=7))
-        rope_bank = ctx.enter_context(tc.psum_pool(name="rope_bank", bufs=1))
+        leaving = ctx.enter_context(tc.tile_pool(name="leaving", bufs=8))
+        leaving_pairs = ctx.enter_context(tc.tile_pool(name="leaving_pairs", bufs=8))
+        banks = ctx.enter_context(tc.psum_pool(name="banks", bufs=8))
         ctx.enter_context(tc.manual_schedule())
 
         wa_raw = [keep.tile([P, PACK, A_COLS], BF16, name="wa_raw%d" % g) for g in range(PASSES)]
         wa_grouped = [
-            keep.tile([P, A_COLS, PACK], BF16, name="wa_grouped%d" % g, align_bytes=64) for g in range(PASSES)
+            keep.tile([P, LATENT, PACK], BF16, name="wa_grouped%d" % g, align_bytes=64) for g in range(PASSES)
         ]
-        wa_codes = keep.tile([P, PASSES, A_COLS], U32, name="wa_codes", align_bytes=64)
-        wa_scales = keep.tile([P, PASSES, A_COLS], U8, name="wa_scales", align_bytes=64)
+        wa_codes = [keep.tile([P, LATENT], U32, name="wa_codes%d" % g, align_bytes=64) for g in range(PASSES)]
+        wa_scales = [keep.tile([P, LATENT], U8, name="wa_scales%d" % g, align_bytes=64) for g in range(PASSES)]
+        wr_grouped = keep.tile([P, PASSES, ROPE, PACK], BF16, name="wr_grouped", align_bytes=64)
+        wr_codes = keep.tile([P, PASSES, ROPE], U32, name="wr_codes", align_bytes=64)
+        wr_scales = keep.tile([P, PASSES, ROPE], U8, name="wr_scales", align_bytes=64)
         x_raw = [keep.tile([P, D_MODEL], BF16, name="x_raw%d" % a) for a in range(TILES)]
         x_grouped = [keep.tile([P, PASSES, P, 2], F32, name="x_grouped%d" % a, align_bytes=64) for a in range(TILES)]
         x_codes = [keep.tile([P, PASSES * P], U32, name="x_codes%d" % a, align_bytes=64) for a in range(TILES)]
         x_scales = [keep.tile([P, PASSES * P], U8, name="x_scales%d" % a, align_bytes=64) for a in range(TILES)]
         sum_squares = [keep.tile([P, 1], F32, name="sum_squares%d" % a) for a in range(TILES)]
-        rms = [keep.tile([P, 1], F32, name="rms%d" % a) for a in range(TILES)]
         inv_rms = [keep.tile([P, 1], F32, name="inv_rms%d" % a) for a in range(TILES)]
         normed = [keep.tile([P, LATENT], BF16, name="normed%d" % a) for a in range(TILES)]
-        n_grouped = [keep.tile([P, P, PACK], BF16, name="n_grouped%d" % a, align_bytes=64) for a in range(TILES)]
+        n_grouped = [keep.tile([P, P, 2], F32, name="n_grouped%d" % a, align_bytes=64) for a in range(TILES)]
         n_codes = [keep.tile([P, P], U32, name="n_codes%d" % a, align_bytes=64) for a in range(TILES)]
         n_scales = [keep.tile([P, P], U8, name="n_scales%d" % a, align_bytes=64) for a in range(TILES)]
-        wb_raw = [keep.tile([P, PACK, CHUNK_COLS], BF16, name="wb_raw%d" % c) for c in range(CHUNKS)]
-        wb_codes = keep.tile([P, PIECES, PIECE_COLS], U32, name="wb_codes", align_bytes=64)
-        wb_scales = keep.tile([P, PIECES, PIECE_COLS], U8, name="wb_scales", align_bytes=64)
-        raw_rope = rope_bank.tile([P, TILES, ROPE], F32, name="raw_rope")
+        wb_raw = [keep.tile([P, PACK, LOAD_COLS[c]], BF16, name="wb_raw%d" % c) for c in range(len(LOAD_COLS))]
+        wb_codes = [keep.tile([P, PIECE_COLS], U32, name="wb_codes%d" % j, align_bytes=64) for j in range(PIECES)]
+        wb_scales = [keep.tile([P, PIECE_COLS], U8, name="wb_scales%d" % j, align_bytes=64) for j in range(PIECES)]
+        out_tiles = {}
         in_psum = {}
         wb_grouped = {}
-
-        eps = keep.tile([P, 1], F32, name="eps")
-        nc.vector.memset(eps[:], RMS_EPS)
-        table_loaded = keep.tile([P, 2], F32, name="table_loaded")
-        nc.scalar.activation(out=table_loaded[:, 0:1], in_=eps[:], func=ACT.Sin)
-        gain_row = keep.tile([P, LATENT], BF16, name="gain_row")
-        nc.vector.memset(gain_row[:], 0.0)
-        position_int = keep.tile([P, SEQ_HALVES], I32, name="position_int")
-        nc.gpsimd.iota(position_int[:], pattern=[[P, SEQ_HALVES]], base=0, channel_multiplier=1)
 
         def load_wa(g):
             nc.sync.dma_start(
@@ -100,19 +96,36 @@ def tile_multiheadlatentattention_pa_kernel(tc, x, Wkv_a, kv_norm_w, Wkv_b, out_
             nc.sync.dma_start(out=x_raw[a][:], in_=x_rows[P * a : P * (a + 1), :])
 
         def load_wb(c):
+            first = sum(LOAD_COLS[:c])
             nc.sync.dma_start(
                 out=wb_raw[c][:],
-                in_=Wkv_b[:, CHUNK_COLS * c : CHUNK_COLS * (c + 1)].rearrange("(p t) n -> p t n", t=PACK),
+                in_=Wkv_b[:, first : first + LOAD_COLS[c]].rearrange("(p t) n -> p t n", t=PACK),
             )
 
-        load_x(0)
-        load_x(1)
-        for g in range(PASSES):
-            load_wa(g)
+        position_int = keep.tile([P, SEQ_HALVES], I32, name="position_int")
+        nc.gpsimd.iota(position_int[:], pattern=[[P, SEQ_HALVES]], base=0, channel_multiplier=1)
+        gain_row = keep.tile([P, LATENT], BF16, name="gain_row")
+        nc.gpsimd.memset(gain_row[:], 0.0)
+        identity_f32 = keep.tile([P, P], F32, name="identity_f32")
+        make_identity(nc, identity_f32[:])
+        ones = keep.tile([P, P], BF16, name="ones")
+        nc.gpsimd.memset(ones[:], 1.0)
+        eps = keep.tile([P, 1], F32, name="eps")
+        nc.vector.memset(eps[:], RMS_EPS)
+        table_loaded = keep.tile([P, 2], F32, name="table_loaded")
+        nc.scalar.activation(out=table_loaded[:, 0:1], in_=eps[:], func=ACT.Sin)
+        gain = keep.tile([P, LATENT], F32, name="gain")
+
+        load_wa(0)
         nc.sync.dma_start(out=gain_row[0:1, :], in_=kv_norm_w.rearrange("(o n) -> o n", o=1))
+        load_x(0)
+        load_wa(1)
+        load_x(1)
+        load_wa(2)
+        load_wa(3)
         load_x(2)
         load_x(3)
-        for c in range(CHUNKS):
+        for c in range(len(LOAD_COLS)):
             load_wb(c)
 
         frequency = keep.tile([P, ROPE_PAIRS], F32, name="frequency")
@@ -145,174 +158,185 @@ def tile_multiheadlatentattention_pa_kernel(tc, x, Wkv_a, kv_norm_w, Wkv_b, out_
         nc.vector.tensor_tensor(out=part_turn[:], in0=turns_row, in1=whole[:], op=ALU.subtract)
         SIN, COS, MINUS_SIN = 0, 1, 2
         trig = keep.tile([P, 3, SEQ_HALVES * ROPE_PAIRS], F32, name="trig")
+        nc.scalar.activation(
+            out=trig[:, SIN : COS + 1, :].rearrange("p s n -> p (s n)"), in_=part_turn[:], func=ACT.Sin, scale=TWO_PI
+        )
+        nc.scalar.activation(out=trig[:, MINUS_SIN, :], in_=part_turn[:, 0:P], func=ACT.Sin, scale=-TWO_PI)
+        nc.scalar.activation(out=table_loaded[:, 1:2], in_=eps[:], func=ACT.Abs_reciprocal_sqrt)
 
-        ones = keep.tile([P, P], BF16, name="ones")
-        nc.vector.memset(ones[:], 1.0)
-        identity_f32 = keep.tile([P, P], F32, name="identity_f32")
-        make_identity(nc, identity_f32[:])
-        identity_bf16 = keep.tile([P, P], BF16, name="identity_bf16")
-        make_identity(nc, identity_bf16[:])
-        gain = keep.tile([P, LATENT], F32, name="gain")
-
-        def rope_tables_scalar():
-            nc.scalar.activation(
-                out=trig[:, SIN : COS + 1, :].rearrange("p s n -> p (s n)"), in_=part_turn[:], func=ACT.Sin, scale=TWO_PI
+        def regroup_wa(g, first, last, copy):
+            copy(
+                out=wa_grouped[g][:, first:last, :].rearrange("p (c i) t -> p c t i", i=RUN),
+                in_=wa_raw[g][:, :, first:last].rearrange("p t (c i) -> p c t i", i=RUN),
             )
-            nc.scalar.activation(out=trig[:, MINUS_SIN, :], in_=part_turn[:, 0:P], func=ACT.Sin, scale=-TWO_PI)
 
-        def load_sqrt_table():
-            nc.scalar.activation(out=table_loaded[:, 1:2], in_=eps[:], func=ACT.Sqrt)
+        def quantise_wa(g):
+            nc.vector.quantize_mx(
+                out=wa_codes[g][:].bitcast(FP8X4),
+                scales=wa_scales[g][:],
+                in_=wa_grouped[g][:].rearrange("p c t -> p (c t)"),
+            )
 
-        def regroup_wa(g):
-            for copy, first, last in (
-                (nc.scalar.copy, WA_VECTOR_COLS, A_COLS),
-                (nc.vector.tensor_copy, 0, WA_VECTOR_COLS),
-            ):
-                copy(
-                    out=wa_grouped[g][:, first:last, :].rearrange("p (c i) t -> p c t i", i=RUN),
-                    in_=wa_raw[g][:, :, first:last].rearrange("p t (c i) -> p c t i", i=RUN),
+        def regroup_wr():
+            for g in range(PASSES):
+                nc.vector.tensor_copy(
+                    out=wr_grouped[:, g, :, :].rearrange("p (c i) t -> p c t i", i=RUN),
+                    in_=wa_raw[g][:, :, LATENT:A_COLS].rearrange("p t (c i) -> p c t i", i=RUN),
                 )
 
-        def quantise_wa(g, first, last):
+        def quantise_wr():
             nc.vector.quantize_mx(
-                out=wa_codes[:, g, first:last].bitcast(FP8X4),
-                scales=wa_scales[:, g, first:last],
-                in_=wa_grouped[g][:, first:last, :].rearrange("p c t -> p (c t)"),
+                out=wr_codes[:].rearrange("p g c -> p (g c)").bitcast(FP8X4),
+                scales=wr_scales[:].rearrange("p g c -> p (g c)"),
+                in_=wr_grouped[:].rearrange("p g c t -> p (g c t)"),
             )
 
-        def spread_gain():
+        def spread_gain(copy):
             summed = banks.tile([P, LATENT], F32, name="summed", tag="bank")
             nc.tensor.matmul(out=summed[:], lhsT=ones[:], rhs=gain_row[:], start=True, stop=True)
-            nc.vector.tensor_copy(out=gain[:], in_=summed[:])
+            copy(out=gain[:], in_=summed[:])
 
-        def transpose_x(a, copy):
+        def transpose_x(a, h):
             words = x_raw[a][:].bitcast(F32)
-            for first_pass in range(0, PASSES, 2):
-                turned = banks.tile([P, 2, 2, P], F32, name="turned", tag="bank")
-                for g in range(2):
-                    for u in range(2):
-                        first_word = 2 * P * (first_pass + g)
-                        nc.tensor.transpose(
-                            turned[:, g, u, :], words[:, first_word + u : first_word + 2 * P : 2], identity_f32[:]
-                        )
-                copy(
-                    out=x_grouped[a][:, first_pass : first_pass + 2, :, :],
-                    in_=turned[:].rearrange("p g u r -> p g r u"),
-                )
+            in_psum["x", a, h] = banks.tile([P, 2, 2, P], F32, name="turned", tag="bank")
+            for g in range(2):
+                for u in range(2):
+                    first_word = 2 * P * (2 * h + g)
+                    nc.tensor.transpose(
+                        in_psum["x", a, h][:, g, u, :], words[:, first_word + u : first_word + 2 * P : 2], identity_f32[:]
+                    )
 
-        def quantise_x(a):
-            for first_pass in range(0, PASSES, 2):
-                columns = slice(P * first_pass, P * (first_pass + 2))
-                nc.vector.quantize_mx(
-                    out=x_codes[a][:, columns].bitcast(FP8X4),
-                    scales=x_scales[a][:, columns],
-                    in_=x_grouped[a][:, first_pass : first_pass + 2, :, :].rearrange("p g r u -> p (g r u)").bitcast(BF16),
-                )
+        def copy_x(a, h, copy):
+            copy(
+                out=x_grouped[a][:, 2 * h : 2 * h + 2, :, :],
+                in_=in_psum["x", a, h][:].rearrange("p g u r -> p g r u"),
+            )
 
-        def first_matmul(a, out, first, last):
-            for g in range(PASSES):
-                nc.tensor.matmul_mx(
-                    out=out,
-                    lhsT=x_codes[a][:, P * g : P * (g + 1)].bitcast(FP8X4),
-                    lhsT_scale=x_scales[a][:, P * g : P * (g + 1)],
-                    rhs=wa_codes[:, g, first:last].bitcast(FP8X4),
-                    rhs_scale=wa_scales[:, g, first:last],
-                    start=(g == 0),
-                    stop=(g == PASSES - 1),
-                )
+        def quantise_x(a, h):
+            columns = slice(2 * P * h, 2 * P * (h + 1))
+            nc.vector.quantize_mx(
+                out=x_codes[a][:, columns].bitcast(FP8X4),
+                scales=x_scales[a][:, columns],
+                in_=x_grouped[a][:, 2 * h : 2 * h + 2, :, :].rearrange("p g r u -> p (g r u)").bitcast(BF16),
+            )
 
-        def latent(a):
-            in_psum["latent", a] = banks.tile([P, LATENT], F32, name="latent", tag="bank")
-            first_matmul(a, in_psum["latent", a][:], 0, LATENT)
+        def latent_pass(a, g):
+            if g == 0:
+                in_psum["latent", a] = banks.tile([P, LATENT], F32, name="latent", tag="bank")
+            nc.tensor.matmul_mx(
+                out=in_psum["latent", a][:],
+                lhsT=x_codes[a][:, P * g : P * (g + 1)].bitcast(FP8X4),
+                lhsT_scale=x_scales[a][:, P * g : P * (g + 1)],
+                rhs=wa_codes[g][:].bitcast(FP8X4),
+                rhs_scale=wa_scales[g][:],
+                start=(g == 0),
+                stop=(g == PASSES - 1),
+            )
+
+        def rope_key():
+            in_psum["rope"] = banks.tile([P, TILES, ROPE], F32, name="raw_rope", tag="bank")
+            for a in range(TILES):
+                for g in range(PASSES):
+                    nc.tensor.matmul_mx(
+                        out=in_psum["rope"][:, a, :],
+                        lhsT=x_codes[a][:, P * g : P * (g + 1)].bitcast(FP8X4),
+                        lhsT_scale=x_scales[a][:, P * g : P * (g + 1)],
+                        rhs=wr_codes[:, g, :].bitcast(FP8X4),
+                        rhs_scale=wr_scales[:, g, :],
+                        start=(g == 0),
+                        stop=(g == PASSES - 1),
+                    )
+
+        def find_rms(a):
             squares = scrap.tile([P, LATENT], BF16, name="squares")
             nc.scalar.activation(out=squares[:], in_=in_psum["latent", a][:], func=ACT.Square, accum_out=sum_squares[a][:])
-            nc.scalar.activation(out=rms[a][:], in_=sum_squares[a][:], func=ACT.Sqrt, scale=1.0 / LATENT, bias=eps[:])
-
-        def rope_key(a):
-            first_matmul(a, raw_rope[:, a, :], LATENT, A_COLS)
+            nc.scalar.activation(
+                out=inv_rms[a][:], in_=sum_squares[a][:], func=ACT.Abs_reciprocal_sqrt, scale=1.0 / LATENT, bias=eps[:]
+            )
 
         def normalise(a):
-            nc.vector.reciprocal(out=inv_rms[a][:], in_=rms[a][:])
             nc.vector.scalar_tensor_tensor(
-                out=normed[a][:].rearrange("p (t q) -> p t q", t=PACK),
-                in0=in_psum["latent", a][:].rearrange("p (q t) -> p t q", t=PACK),
+                out=normed[a][:],
+                in0=in_psum["latent", a][:],
                 scalar=inv_rms[a][:],
-                in1=gain[:].rearrange("p (q t) -> p t q", t=PACK),
+                in1=gain[:],
                 op0=ALU.mult,
                 op1=ALU.mult,
             )
 
-        def transpose_n(a, copy):
-            turned = banks.tile([P, PACK, P], BF16, name="turned_n", tag="bank")
-            for t in range(PACK):
-                nc.tensor.transpose(turned[:, t, :], normed[a][:, P * t : P * (t + 1)], identity_bf16[:])
-            copy(out=n_grouped[a][:], in_=turned[:].rearrange("p t r -> p r t"))
+        def transpose_n(a):
+            words = normed[a][:].bitcast(F32)
+            in_psum["n", a] = banks.tile([P, 2, P], F32, name="turned_n", tag="bank")
+            for u in range(2):
+                nc.tensor.transpose(in_psum["n", a][:, u, :], words[:, u : 2 * P : 2], identity_f32[:])
+
+        def copy_n(a, copy):
+            copy(out=n_grouped[a][:], in_=in_psum["n", a][:].rearrange("p u r -> p r u"))
 
         def quantise_n(a):
             nc.vector.quantize_mx(
                 out=n_codes[a][:].bitcast(FP8X4),
                 scales=n_scales[a][:],
-                in_=n_grouped[a][:].rearrange("p r t -> p (r t)"),
+                in_=n_grouped[a][:].rearrange("p r u -> p (r u)").bitcast(BF16),
             )
 
-        def regroup_wb(j):
-            wb_grouped[j] = regrouped.tile([P, PIECE_COLS, PACK], BF16, name="wb_grouped", align_bytes=64)
-            by_head = wb_raw[j // 2][:].rearrange(
-                "p t (h k c i) -> p t h k c i", h=CHUNK_HEADS, k=2, c=HEAD_DIM // RUN, i=RUN
-            )
-            nc.vector.tensor_copy(
-                out=wb_grouped[j][:].rearrange("p (h c i) t -> p h c t i", h=CHUNK_HEADS, c=HEAD_DIM // RUN, i=RUN),
-                in_=by_head[:, :, :, j % 2, :, :].rearrange("p t h c i -> p h c t i"),
+        def regroup_wb(j, first, last, copy):
+            if j not in wb_grouped:
+                wb_grouped[j] = regrouped.tile([P, PIECE_COLS, PACK], BF16, name="wb_grouped", align_bytes=64)
+            to_heads = wb_grouped[j][:].rearrange("p (h c i) t -> p h c t i", h=CHUNK_HEADS, i=RUN)
+            chunk, kind = PIECE_ORDER[j]
+            load = min(chunk, len(LOAD_COLS) - 1)
+            head = CHUNK_HEADS * (chunk - load)
+            from_heads = wb_raw[load][:].rearrange("p t (h k c i) -> p t h k c i", k=2, c=HEAD_DIM // RUN, i=RUN)
+            copy(
+                out=to_heads[:, first:last],
+                in_=from_heads[:, :, head + first : head + last, kind, :, :].rearrange("p t h c i -> p h c t i"),
             )
 
         def quantise_wb(j):
             nc.vector.quantize_mx(
-                out=wb_codes[:, j, :].bitcast(FP8X4),
-                scales=wb_scales[:, j, :],
+                out=wb_codes[j][:].bitcast(FP8X4),
+                scales=wb_scales[j][:],
                 in_=wb_grouped[j][:].rearrange("p c t -> p (c t)"),
             )
 
-        def second_matmul(a, j):
+        def product(a, j):
             in_psum["kv", a, j] = banks.tile([P, PIECE_COLS], F32, name="kv", tag="bank")
             nc.tensor.matmul_mx(
                 out=in_psum["kv", a, j][:],
                 lhsT=n_codes[a][:].bitcast(FP8X4),
                 lhsT_scale=n_scales[a][:],
-                rhs=wb_codes[:, j, :].bitcast(FP8X4),
-                rhs_scale=wb_scales[:, j, :],
+                rhs=wb_codes[j][:].bitcast(FP8X4),
+                rhs_scale=wb_scales[j][:],
                 start=True,
                 stop=True,
             )
 
-        def store_kv(a, j):
-            out_tile = leaving.tile([P, PIECE_COLS], F32, name="out_tile")
-            if j == PIECES - 1 and a % 2 == 1:
-                nc.vector.tensor_copy(out=out_tile[:], in_=in_psum["kv", a, j][:])
-            else:
-                nc.scalar.copy(out=out_tile[:], in_=in_psum["kv", a, j][:])
-            nc.sync.dma_start(
-                out=kv_out[j % 2][P * a : P * (a + 1), PIECE_COLS * (j // 2) : PIECE_COLS * (j // 2 + 1)],
-                in_=out_tile[:],
-            )
+        def leave(a, j, copy):
+            chunk, kind = PIECE_ORDER[j]
+            pair = j >= FIRST_PAIRED
+            if pair and chunk % 2 == 0:
+                out_tiles[a] = leaving_pairs.tile([P, 2, PIECE_COLS], F32, name="out_pair")
+            elif not pair:
+                out_tiles[a] = leaving.tile([P, 1, PIECE_COLS], F32, name="out_tile")
+            part = chunk % 2 if pair else 0
+            copy(out=out_tiles[a][:, part, :], in_=in_psum["kv", a, j][:])
+            if not pair or part == 1:
+                nc.sync.dma_start(
+                    out=kv_out[kind][P * a : P * (a + 1), PIECE_COLS * (chunk - part) : PIECE_COLS * (chunk + 1)],
+                    in_=out_tiles[a][:].rearrange("p s c -> p (s c)"),
+                )
 
-        def kv(products):
-            for a, j in products:
-                second_matmul(a, j)
-            for a, j in products:
-                store_kv(a, j)
-
-        pairs = raw_rope[:].rearrange("p (b h) (i e) -> p b (h i) e", b=2, e=2)
         both = [P, 2, P]
         by_cos = keep.tile([P, 2, P, 2], F32, name="by_cos")
         by_sin = keep.tile([P, 2, 2, P], F32, name="by_sin")
         k_rope = keep.tile([P, 2, P, 2], F32, name="k_rope")
 
-        def rope_by_cos():
+        def rope_products():
+            pairs = in_psum["rope"][:].rearrange("p (b h) (i e) -> p b (h i) e", b=2, e=2)
             nc.vector.tensor_tensor(
                 out=by_cos[:], in0=pairs, in1=trig[:, COS, :].unsqueeze(1).unsqueeze(3).to_broadcast([P, 2, P, 2]), op=ALU.mult
             )
-
-        def rope_by_sin():
             nc.vector.tensor_tensor(
                 out=by_sin[:, 0, :, :], in0=pairs[:, :, :, 1], in1=trig[:, MINUS_SIN, :].unsqueeze(1).to_broadcast(both), op=ALU.mult
             )
@@ -324,76 +348,135 @@ def tile_multiheadlatentattention_pa_kernel(tc, x, Wkv_a, kv_norm_w, Wkv_b, out_
             nc.vector.tensor_tensor(
                 out=k_rope[:], in0=by_cos[:], in1=by_sin[:].rearrange("p e b n -> p b n e"), op=ALU.add
             )
+
+        def store_rope():
             nc.sync.dma_start(
                 out=out_2.rearrange("b (h p) o d -> p (b h) (o d)", h=SEQ_HALVES, p=P),
                 in_=k_rope[:].rearrange("p b (h i) e -> p (b h) (i e)", h=SEQ_HALVES),
             )
 
-        transpose_x(0, nc.scalar.copy)
-        transpose_x(1, nc.scalar.copy)
-        quantise_x(0)
-        regroup_wa(0)
-        quantise_x(1)
-        for g in range(PASSES):
-            if g + 1 < PASSES:
-                regroup_wa(g + 1)
-            if g == PASSES - 2:
-                spread_gain()
-            quantise_wa(g, 0, LATENT)
-        rope_tables_scalar()
-        load_sqrt_table()
+        vector, scalar = nc.vector.tensor_copy, nc.scalar.copy
 
-        transpose_x(2, nc.vector.tensor_copy)
-        transpose_x(3, nc.scalar.copy)
-        quantise_x(2)
-        regroup_wb(0)
-        quantise_x(3)
-
-        for a in range(TILES):
-            latent(a)
+        half = LATENT // 2
+        regroup_wa(0, 0, LATENT, vector)
+        spread_gain(scalar)
+        quantise_wa(0)
+        transpose_x(0, 0)
+        copy_x(0, 0, scalar)
+        transpose_x(0, 1)
+        regroup_wa(1, 0, half, vector)
+        regroup_wa(1, half, LATENT, scalar)
+        copy_x(0, 1, scalar)
+        quantise_x(0, 0)
+        quantise_wa(1)
+        quantise_x(0, 1)
+        for h in range(2):
+            transpose_x(1, h)
+        latent_pass(0, 0)
+        latent_pass(0, 1)
+        copy_x(1, 0, scalar)
+        regroup_wa(2, 0, half, vector)
+        regroup_wa(2, half, LATENT, scalar)
+        copy_x(1, 1, scalar)
+        quantise_x(1, 0)
+        regroup_wa(3, 0, WA_VECTOR_COLS, vector)
+        regroup_wa(3, WA_VECTOR_COLS, LATENT, scalar)
+        quantise_wa(2)
+        quantise_wa(3)
+        quantise_x(1, 1)
+        latent_pass(1, 0)
+        latent_pass(1, 1)
+        for h in range(2):
+            transpose_x(2, h)
+        for g in (2, 3):
+            latent_pass(0, g)
+        for g in (2, 3):
+            latent_pass(1, g)
+        for h in range(2):
+            transpose_x(3, h)
+        copy_x(2, 0, scalar)
+        find_rms(0)
+        copy_x(2, 1, vector)
+        quantise_x(2, 0)
+        find_rms(1)
         normalise(0)
-        quantise_wb(0)
+        quantise_x(2, 1)
+        transpose_n(0)
+        copy_n(0, scalar)
+        copy_x(3, 0, scalar)
         normalise(1)
-        regroup_wb(1)
-        normalise(2)
-        quantise_wb(1)
-        for a in range(TILES - 1):
-            transpose_n(a, nc.scalar.copy)
+        transpose_n(1)
+        for g in range(PASSES):
+            latent_pass(2, g)
+        copy_n(1, scalar)
+        copy_x(3, 1, scalar)
+        regroup_wb(0, 0, CHUNK_HEADS, vector)
+        find_rms(2)
         quantise_n(0)
         quantise_n(1)
-        regroup_wb(2)
-        quantise_n(2)
-        normalise(3)
-        quantise_wb(2)
-        regroup_wb(3)
-
-        early = ((0, 0), (1, 0), (0, 1), (1, 1), (2, 0), (2, 1))
-        for a, j in early:
-            second_matmul(a, j)
-        transpose_n(TILES - 1, nc.vector.tensor_copy)
-        quantise_n(TILES - 1)
-        for a, j in early:
-            store_kv(a, j)
-        quantise_wb(3)
-        regroup_wb(4)
-        quantise_wb(4)
-        kv(((0, 2), (1, 2), (2, 2)))
-        kv(((3, 0), (3, 1), (3, 2)))
-
+        quantise_wb(0)
+        product(0, 0)
+        product(1, 0)
+        quantise_x(3, 0)
+        quantise_x(3, 1)
         for g in range(PASSES):
-            quantise_wa(g, LATENT, A_COLS)
-        for j in range(5, PIECES - 1):
-            regroup_wb(j)
-            quantise_wb(j)
-        regroup_wb(PIECES - 1)
-
-        for j in range(3, PIECES):
-            if j == 5:
-                for a in range(TILES):
-                    rope_key(a)
-            if j == PIECES - 1:
-                rope_by_cos()
-                rope_by_sin()
-                rope_sum()
-                quantise_wb(j)
-            kv([(a, j) for a in range(TILES)])
+            latent_pass(3, g)
+        regroup_wb(1, CHUNK_HEADS // 2, CHUNK_HEADS, scalar)
+        leave(0, 0, scalar)
+        find_rms(3)
+        leave(1, 0, scalar)
+        regroup_wb(1, 0, CHUNK_HEADS // 2, vector)
+        normalise(2)
+        quantise_wb(1)
+        normalise(3)
+        transpose_n(2)
+        product(0, 1)
+        product(1, 1)
+        transpose_n(3)
+        copy_n(2, scalar)
+        leave(0, 1, scalar)
+        copy_n(3, scalar)
+        leave(1, 1, scalar)
+        regroup_wb(2, 0, CHUNK_HEADS, vector)
+        quantise_n(2)
+        quantise_n(3)
+        quantise_wb(2)
+        for a in (2, 3):
+            for j in (0, 1):
+                product(a, j)
+        for a in (2, 3):
+            for j in (0, 1):
+                leave(a, j, scalar)
+        for j in (2, 3):
+            regroup_wb(j + 1, 0, CHUNK_HEADS, vector)
+            quantise_wb(j + 1)
+            for a in range(TILES):
+                product(a, j)
+            for a in range(TILES):
+                leave(a, j, scalar)
+        regroup_wb(5, 0, CHUNK_HEADS, vector)
+        quantise_wb(5)
+        for a in range(TILES):
+            for j in (4, 5):
+                product(a, j)
+        for a in range(TILES):
+            for j in (4, 5):
+                leave(a, j, scalar)
+        regroup_wb(6, 0, CHUNK_HEADS, vector)
+        quantise_wb(6)
+        regroup_wb(7, 0, CHUNK_HEADS, vector)
+        quantise_wb(7)
+        regroup_wr()
+        quantise_wr()
+        for a in range(TILES):
+            if a == 2:
+                rope_key()
+            for j in (6, 7):
+                product(a, j)
+        rope_products()
+        rope_sum()
+        for a in range(TILES):
+            for j in (6, 7):
+                leave(a, j, vector if a == TILES - 1 else scalar)
+            if a == TILES - 2:
+                store_rope()

@@ -57,7 +57,8 @@ def tile_multiheadlatentattention_pa_kernel(tc, x, Wkv_a, kv_norm_w, Wkv_b, out_
         scrap = ctx.enter_context(tc.tile_pool(name="scrap", bufs=2))
         leaving = ctx.enter_context(tc.tile_pool(name="leaving", bufs=8))
         leaving_pairs = ctx.enter_context(tc.tile_pool(name="leaving_pairs", bufs=8))
-        banks = ctx.enter_context(tc.psum_pool(name="banks", bufs=8))
+        banks = ctx.enter_context(tc.psum_pool(name="banks", bufs=7))
+        idle_bank = ctx.enter_context(tc.psum_pool(name="idle_bank", bufs=1))
         ctx.enter_context(tc.manual_schedule())
 
         wa_raw = [keep.tile([P, PACK, A_COLS], BF16, name="wa_raw%d" % g) for g in range(PASSES)]
@@ -102,67 +103,69 @@ def tile_multiheadlatentattention_pa_kernel(tc, x, Wkv_a, kv_norm_w, Wkv_b, out_
                 in_=Wkv_b[:, first : first + LOAD_COLS[c]].rearrange("(p t) n -> p t n", t=PACK),
             )
 
-        position_int = keep.tile([P, SEQ_HALVES], I32, name="position_int")
-        nc.gpsimd.iota(position_int[:], pattern=[[P, SEQ_HALVES]], base=0, channel_multiplier=1)
         gain_row = keep.tile([P, LATENT], BF16, name="gain_row")
-        nc.gpsimd.memset(gain_row[:], 0.0)
+        nc.vector.memset(gain_row[:], 0.0)
+        position = keep.tile([P, SEQ_HALVES], I32, name="position")
+        nc.gpsimd.iota(position[:], pattern=[[P, SEQ_HALVES]], base=0, channel_multiplier=1)
         identity_f32 = keep.tile([P, P], F32, name="identity_f32")
         make_identity(nc, identity_f32[:])
         ones = keep.tile([P, P], BF16, name="ones")
-        nc.gpsimd.memset(ones[:], 1.0)
+        nc.vector.memset(ones[:], 1.0)
+        zeros = keep.tile([P, LATENT], BF16, name="zeros")
+        nc.vector.memset(zeros[:], 0.0)
         eps = keep.tile([P, 1], F32, name="eps")
         nc.vector.memset(eps[:], RMS_EPS)
         table_loaded = keep.tile([P, 2], F32, name="table_loaded")
         nc.scalar.activation(out=table_loaded[:, 0:1], in_=eps[:], func=ACT.Sin)
-        gain = keep.tile([P, LATENT], F32, name="gain")
 
         load_wa(0)
         nc.sync.dma_start(out=gain_row[0:1, :], in_=kv_norm_w.rearrange("(o n) -> o n", o=1))
         load_x(0)
-        load_wa(1)
         load_x(1)
-        load_wa(2)
-        load_wa(3)
+        load_wa(1)
         load_x(2)
+        load_wa(2)
         load_x(3)
-        for c in range(len(LOAD_COLS)):
-            load_wb(c)
+        load_wa(3)
+        load_wb(0)
+        load_wb(1)
+        load_wb(2)
 
-        frequency = keep.tile([P, ROPE_PAIRS], F32, name="frequency")
-        nc.vector.memset(frequency[:, 0:1], 1.0)
-        for filled in (1, 2, 4, 8, 16, 32):
-            nc.vector.tensor_scalar_mul(
-                out=frequency[:, filled : 2 * filled],
-                in0=frequency[:, 0:filled],
-                scalar1=ROPE_BASE ** (-2.0 * filled / ROPE),
+        turns = keep.tile([P, ROPE_PAIRS, SEQ_HALVES], F32, name="turns")
+        nc.vector.tensor_scalar_mul(out=turns[:, 0, :], in0=position[:], scalar1=1.0 / TWO_PI)
+        for filled in (1, 4, 16):
+            for run in (1, 2, 3):
+                nc.vector.tensor_scalar_mul(
+                    out=turns[:, run * filled : (run + 1) * filled, :],
+                    in0=turns[:, 0:filled, :],
+                    scalar1=ROPE_BASE ** (-2.0 * run * filled / ROPE),
+                )
+        QUARTER = (0.0, 0.25)
+        whole = keep.tile([P, 2, SEQ_HALVES, ROPE_PAIRS], I32, name="whole")
+        part_turn = keep.tile([P, 2, SEQ_HALVES, ROPE_PAIRS], F32, name="part_turn")
+        half_by_half = turns[:].rearrange("p i h -> p h i")
+        for s in range(2):
+            nc.vector.tensor_scalar_add(out=whole[:, s, :, :], in0=half_by_half, scalar1=QUARTER[s])
+        for s in range(2):
+            nc.vector.scalar_tensor_tensor(
+                out=part_turn[:, s, :, :],
+                in0=half_by_half,
+                scalar=QUARTER[s],
+                in1=whole[:, s, :, :],
+                op0=ALU.add,
+                op1=ALU.subtract,
             )
-        position = keep.tile([P, SEQ_HALVES], F32, name="position")
-        nc.vector.tensor_copy(out=position[:], in_=position_int[:])
-        turns = keep.tile([P, 2, SEQ_HALVES, ROPE_PAIRS], F32, name="turns")
-        for half in range(SEQ_HALVES):
-            nc.vector.tensor_scalar(
-                out=turns[:, 0, half, :],
-                in0=frequency[:],
-                scalar1=position[:, half : half + 1],
-                scalar2=1.0 / TWO_PI,
-                op0=ALU.mult,
-                op1=ALU.mult,
-            )
-        nc.vector.tensor_scalar_add(out=turns[:, 1, :, :], in0=turns[:, 0, :, :], scalar1=0.25)
-        turns_row = turns[:].rearrange("p s h i -> p (s h i)")
-        whole_int = keep.tile([P, 2 * P], I32, name="whole_int")
-        nc.vector.tensor_copy(out=whole_int[:], in_=turns_row)
-        whole = keep.tile([P, 2 * P], F32, name="whole")
-        nc.vector.tensor_copy(out=whole[:], in_=whole_int[:])
-        part_turn = keep.tile([P, 2 * P], F32, name="part_turn")
-        nc.vector.tensor_tensor(out=part_turn[:], in0=turns_row, in1=whole[:], op=ALU.subtract)
         SIN, COS, MINUS_SIN = 0, 1, 2
         trig = keep.tile([P, 3, SEQ_HALVES * ROPE_PAIRS], F32, name="trig")
-        nc.scalar.activation(
-            out=trig[:, SIN : COS + 1, :].rearrange("p s n -> p (s n)"), in_=part_turn[:], func=ACT.Sin, scale=TWO_PI
-        )
-        nc.scalar.activation(out=trig[:, MINUS_SIN, :], in_=part_turn[:, 0:P], func=ACT.Sin, scale=-TWO_PI)
+        for out, angle, sign in ((SIN, SIN, 1.0), (COS, COS, 1.0), (MINUS_SIN, SIN, -1.0)):
+            nc.scalar.activation(
+                out=trig[:, out, :],
+                in_=part_turn[:, angle, :, :].rearrange("p h i -> p (h i)"),
+                func=ACT.Sin,
+                scale=sign * TWO_PI,
+            )
         nc.scalar.activation(out=table_loaded[:, 1:2], in_=eps[:], func=ACT.Abs_reciprocal_sqrt)
+        gain = keep.tile([P, LATENT], F32, name="gain")
 
         def regroup_wa(g, first, last, copy):
             copy(
@@ -177,12 +180,11 @@ def tile_multiheadlatentattention_pa_kernel(tc, x, Wkv_a, kv_norm_w, Wkv_b, out_
                 in_=wa_grouped[g][:].rearrange("p c t -> p (c t)"),
             )
 
-        def regroup_wr():
-            for g in range(PASSES):
-                nc.vector.tensor_copy(
-                    out=wr_grouped[:, g, :, :].rearrange("p (c i) t -> p c t i", i=RUN),
-                    in_=wa_raw[g][:, :, LATENT:A_COLS].rearrange("p t (c i) -> p c t i", i=RUN),
-                )
+        def regroup_wr(g, copy):
+            copy(
+                out=wr_grouped[:, g, :, :].rearrange("p (c i) t -> p c t i", i=RUN),
+                in_=wa_raw[g][:, :, LATENT:A_COLS].rearrange("p t (c i) -> p c t i", i=RUN),
+            )
 
         def quantise_wr():
             nc.vector.quantize_mx(
@@ -190,6 +192,12 @@ def tile_multiheadlatentattention_pa_kernel(tc, x, Wkv_a, kv_norm_w, Wkv_b, out_
                 scales=wr_scales[:].rearrange("p g c -> p (g c)"),
                 in_=wr_grouped[:].rearrange("p g c t -> p (g c t)"),
             )
+
+        unread = idle_bank.tile([P, LATENT], F32, name="unread")
+
+        def keep_clock(times):
+            for repeat in range(times):
+                nc.tensor.matmul(out=unread[:], lhsT=ones[:], rhs=zeros[:], start=True, stop=True)
 
         def spread_gain(copy):
             summed = banks.tile([P, LATENT], F32, name="summed", tag="bank")
@@ -212,12 +220,11 @@ def tile_multiheadlatentattention_pa_kernel(tc, x, Wkv_a, kv_norm_w, Wkv_b, out_
                 in_=in_psum["x", a, h][:].rearrange("p g u r -> p g r u"),
             )
 
-        def quantise_x(a, h):
-            columns = slice(2 * P * h, 2 * P * (h + 1))
+        def quantise_x(a):
             nc.vector.quantize_mx(
-                out=x_codes[a][:, columns].bitcast(FP8X4),
-                scales=x_scales[a][:, columns],
-                in_=x_grouped[a][:, 2 * h : 2 * h + 2, :, :].rearrange("p g r u -> p (g r u)").bitcast(BF16),
+                out=x_codes[a][:].bitcast(FP8X4),
+                scales=x_scales[a][:],
+                in_=x_grouped[a][:].rearrange("p g r u -> p (g r u)").bitcast(BF16),
             )
 
         def latent_pass(a, g):
@@ -247,9 +254,11 @@ def tile_multiheadlatentattention_pa_kernel(tc, x, Wkv_a, kv_norm_w, Wkv_b, out_
                         stop=(g == PASSES - 1),
                     )
 
-        def find_rms(a):
+        def sum_of_squares(a):
             squares = scrap.tile([P, LATENT], BF16, name="squares")
             nc.scalar.activation(out=squares[:], in_=in_psum["latent", a][:], func=ACT.Square, accum_out=sum_squares[a][:])
+
+        def find_inv_rms(a):
             nc.scalar.activation(
                 out=inv_rms[a][:], in_=sum_squares[a][:], func=ACT.Abs_reciprocal_sqrt, scale=1.0 / LATENT, bias=eps[:]
             )
@@ -358,103 +367,102 @@ def tile_multiheadlatentattention_pa_kernel(tc, x, Wkv_a, kv_norm_w, Wkv_b, out_
         vector, scalar = nc.vector.tensor_copy, nc.scalar.copy
 
         half = LATENT // 2
+        keep_clock(4)
+        spread_gain(vector)
         regroup_wa(0, 0, LATENT, vector)
-        spread_gain(scalar)
         quantise_wa(0)
-        transpose_x(0, 0)
-        copy_x(0, 0, scalar)
-        transpose_x(0, 1)
-        regroup_wa(1, 0, half, vector)
-        regroup_wa(1, half, LATENT, scalar)
-        copy_x(0, 1, scalar)
-        quantise_x(0, 0)
+        for a in (0, 1):
+            keep_clock(1)
+            for h in range(2):
+                transpose_x(a, h)
+                copy_x(a, h, scalar)
+            regroup_wr(a, scalar)
+        quantise_x(0)
+        regroup_wa(1, 0, LATENT, vector)
+        quantise_x(1)
         quantise_wa(1)
-        quantise_x(0, 1)
-        for h in range(2):
-            transpose_x(1, h)
-        latent_pass(0, 0)
-        latent_pass(0, 1)
-        copy_x(1, 0, scalar)
-        regroup_wa(2, 0, half, vector)
-        regroup_wa(2, half, LATENT, scalar)
-        copy_x(1, 1, scalar)
-        quantise_x(1, 0)
-        regroup_wa(3, 0, WA_VECTOR_COLS, vector)
-        regroup_wa(3, WA_VECTOR_COLS, LATENT, scalar)
-        quantise_wa(2)
-        quantise_wa(3)
-        quantise_x(1, 1)
-        latent_pass(1, 0)
-        latent_pass(1, 1)
+        keep_clock(1)
         for h in range(2):
             transpose_x(2, h)
-        for g in (2, 3):
-            latent_pass(0, g)
-        for g in (2, 3):
-            latent_pass(1, g)
+            copy_x(2, h, scalar)
+        for a in (0, 1):
+            for g in (0, 1):
+                latent_pass(a, g)
+        regroup_wa(2, 0, half, vector)
+        regroup_wa(2, half, LATENT, scalar)
+        quantise_x(2)
+        regroup_wr(2, scalar)
+        quantise_wa(2)
         for h in range(2):
             transpose_x(3, h)
-        copy_x(2, 0, scalar)
-        find_rms(0)
-        copy_x(2, 1, vector)
-        quantise_x(2, 0)
-        find_rms(1)
-        normalise(0)
-        quantise_x(2, 1)
-        transpose_n(0)
-        copy_n(0, scalar)
-        copy_x(3, 0, scalar)
-        normalise(1)
-        transpose_n(1)
-        for g in range(PASSES):
+            copy_x(3, h, scalar)
+        for g in (0, 1):
             latent_pass(2, g)
-        copy_n(1, scalar)
-        copy_x(3, 1, scalar)
-        regroup_wb(0, 0, CHUNK_HEADS, vector)
-        find_rms(2)
-        quantise_n(0)
-        quantise_n(1)
-        quantise_wb(0)
-        product(0, 0)
-        product(1, 0)
-        quantise_x(3, 0)
-        quantise_x(3, 1)
+        for a in (0, 1, 2):
+            latent_pass(a, 2)
+        regroup_wa(3, 0, LATENT, vector)
+        regroup_wr(3, scalar)
+        quantise_wa(3)
+        for a in (0, 1, 2):
+            latent_pass(a, 3)
+        quantise_x(3)
         for g in range(PASSES):
             latent_pass(3, g)
-        regroup_wb(1, CHUNK_HEADS // 2, CHUNK_HEADS, scalar)
-        leave(0, 0, scalar)
-        find_rms(3)
-        leave(1, 0, scalar)
-        regroup_wb(1, 0, CHUNK_HEADS // 2, vector)
+        sum_of_squares(0)
+        sum_of_squares(1)
+        find_inv_rms(0)
+        find_inv_rms(1)
+        sum_of_squares(2)
+        regroup_wb(0, 0, CHUNK_HEADS, vector)
+        normalise(0)
+        transpose_n(0)
+        keep_clock(1)
+        copy_n(0, scalar)
+        sum_of_squares(3)
+        find_inv_rms(2)
+        find_inv_rms(3)
+        quantise_wb(0)
+        normalise(1)
+        transpose_n(1)
+        keep_clock(1)
+        copy_n(1, scalar)
+        quantise_n(0)
+        product(0, 0)
         normalise(2)
-        quantise_wb(1)
-        normalise(3)
         transpose_n(2)
-        product(0, 1)
-        product(1, 1)
+        keep_clock(1)
+        quantise_n(1)
+        product(1, 0)
+        normalise(3)
         transpose_n(3)
+        keep_clock(1)
         copy_n(2, scalar)
-        leave(0, 1, scalar)
+        leave(0, 0, scalar)
         copy_n(3, scalar)
-        leave(1, 1, scalar)
-        regroup_wb(2, 0, CHUNK_HEADS, vector)
+        leave(1, 0, scalar)
+        regroup_wb(1, 0, CHUNK_HEADS, vector)
         quantise_n(2)
+        product(2, 0)
         quantise_n(3)
+        product(3, 0)
+        leave(2, 0, scalar)
+        leave(3, 0, scalar)
+        quantise_wb(1)
+        for a in range(TILES):
+            product(a, 1)
+        regroup_wb(2, 0, CHUNK_HEADS, vector)
+        for a in range(TILES):
+            leave(a, 1, scalar)
         quantise_wb(2)
-        for a in (2, 3):
-            for j in (0, 1):
-                product(a, j)
-        for a in (2, 3):
-            for j in (0, 1):
-                leave(a, j, scalar)
+        regroup_wb(3, 0, CHUNK_HEADS, vector)
         for j in (2, 3):
-            regroup_wb(j + 1, 0, CHUNK_HEADS, vector)
+            regroup_wb(j + 2, 0, CHUNK_HEADS, vector)
             quantise_wb(j + 1)
             for a in range(TILES):
                 product(a, j)
             for a in range(TILES):
                 leave(a, j, scalar)
-        regroup_wb(5, 0, CHUNK_HEADS, vector)
+        regroup_wb(6, 0, CHUNK_HEADS, vector)
         quantise_wb(5)
         for a in range(TILES):
             for j in (4, 5):
@@ -462,18 +470,15 @@ def tile_multiheadlatentattention_pa_kernel(tc, x, Wkv_a, kv_norm_w, Wkv_b, out_
         for a in range(TILES):
             for j in (4, 5):
                 leave(a, j, scalar)
-        regroup_wb(6, 0, CHUNK_HEADS, vector)
-        quantise_wb(6)
-        regroup_wb(7, 0, CHUNK_HEADS, vector)
-        quantise_wb(7)
-        regroup_wr()
         quantise_wr()
+        rope_key()
+        regroup_wb(7, 0, CHUNK_HEADS, vector)
+        quantise_wb(6)
+        quantise_wb(7)
+        rope_products()
         for a in range(TILES):
-            if a == 2:
-                rope_key()
             for j in (6, 7):
                 product(a, j)
-        rope_products()
         rope_sum()
         for a in range(TILES):
             for j in (6, 7):

@@ -55,7 +55,7 @@ def tile_multiheadlatentattention_pa_kernel(tc, x, Wkv_a, kv_norm_w, Wkv_b, out_
         keep = ctx.enter_context(tc.tile_pool(name="keep", bufs=1))
         regrouped = ctx.enter_context(tc.tile_pool(name="regrouped", bufs=3))
         scrap = ctx.enter_context(tc.tile_pool(name="scrap", bufs=2))
-        leaving = ctx.enter_context(tc.tile_pool(name="leaving", bufs=8))
+        leaving = ctx.enter_context(tc.tile_pool(name="leaving", bufs=10))
         leaving_pairs = ctx.enter_context(tc.tile_pool(name="leaving_pairs", bufs=8))
         banks = ctx.enter_context(tc.psum_pool(name="banks", bufs=7))
         idle_bank = ctx.enter_context(tc.psum_pool(name="idle_bank", bufs=1))
@@ -74,12 +74,12 @@ def tile_multiheadlatentattention_pa_kernel(tc, x, Wkv_a, kv_norm_w, Wkv_b, out_
         x_grouped = [keep.tile([P, PASSES, P, 2], F32, name="x_grouped%d" % a, align_bytes=64) for a in range(TILES)]
         x_codes = [keep.tile([P, PASSES * P], U32, name="x_codes%d" % a, align_bytes=64) for a in range(TILES)]
         x_scales = [keep.tile([P, PASSES * P], U8, name="x_scales%d" % a, align_bytes=64) for a in range(TILES)]
-        sum_squares = [keep.tile([P, 1], F32, name="sum_squares%d" % a) for a in range(TILES)]
-        inv_rms = [keep.tile([P, 1], F32, name="inv_rms%d" % a) for a in range(TILES)]
+        sum_squares = keep.tile([P, TILES], F32, name="sum_squares")
+        inv_rms = keep.tile([P, TILES], F32, name="inv_rms")
         normed = [keep.tile([P, LATENT], BF16, name="normed%d" % a) for a in range(TILES)]
-        n_grouped = [keep.tile([P, P, 2], F32, name="n_grouped%d" % a, align_bytes=64) for a in range(TILES)]
-        n_codes = [keep.tile([P, P], U32, name="n_codes%d" % a, align_bytes=64) for a in range(TILES)]
-        n_scales = [keep.tile([P, P], U8, name="n_scales%d" % a, align_bytes=64) for a in range(TILES)]
+        n_grouped = keep.tile([P, TILES, P, 2], F32, name="n_grouped", align_bytes=64)
+        n_codes = keep.tile([P, TILES, P], U32, name="n_codes", align_bytes=64)
+        n_scales = keep.tile([P, TILES, P], U8, name="n_scales", align_bytes=64)
         wb_raw = [keep.tile([P, PACK, LOAD_COLS[c]], BF16, name="wb_raw%d" % c) for c in range(len(LOAD_COLS))]
         wb_codes = [keep.tile([P, PIECE_COLS], U32, name="wb_codes%d" % j, align_bytes=64) for j in range(PIECES)]
         wb_scales = [keep.tile([P, PIECE_COLS], U8, name="wb_scales%d" % j, align_bytes=64) for j in range(PIECES)]
@@ -109,6 +109,8 @@ def tile_multiheadlatentattention_pa_kernel(tc, x, Wkv_a, kv_norm_w, Wkv_b, out_
         nc.gpsimd.iota(position[:], pattern=[[P, SEQ_HALVES]], base=0, channel_multiplier=1)
         identity_f32 = keep.tile([P, P], F32, name="identity_f32")
         make_identity(nc, identity_f32[:])
+        identity_bf16 = keep.tile([P, P], BF16, name="identity_bf16")
+        nc.gpsimd.tensor_copy(out=identity_bf16[:], in_=identity_f32[:])
         ones = keep.tile([P, P], BF16, name="ones")
         nc.vector.memset(ones[:], 1.0)
         zeros = keep.tile([P, LATENT], BF16, name="zeros")
@@ -172,6 +174,23 @@ def tile_multiheadlatentattention_pa_kernel(tc, x, Wkv_a, kv_norm_w, Wkv_b, out_
                 out=wa_grouped[g][:, first:last, :].rearrange("p (c i) t -> p c t i", i=RUN),
                 in_=wa_raw[g][:, :, first:last].rearrange("p t (c i) -> p c t i", i=RUN),
             )
+
+        def regroup_by_tensor(rows):
+            bank = banks.tile([P, 2, HEAD_DIM, PACK], BF16, name="regrouped_rows", tag="bank")
+            for h in range(2):
+                nc.tensor.matmul(
+                    out=bank[:, h, :, :],
+                    lhsT=identity_bf16[:],
+                    rhs=rows(h).rearrange("p t c -> p c t"),
+                    start=True,
+                    stop=True,
+                )
+            return bank[:].rearrange("p h c t -> p (h c) t")
+
+        def regroup_wa_half(g):
+            half = LATENT // 2
+            bank = regroup_by_tensor(lambda h: wa_raw[g][:, :, half + HEAD_DIM * h : half + HEAD_DIM * (h + 1)])
+            nc.scalar.copy(out=wa_grouped[g][:, half:LATENT, :], in_=bank)
 
         def quantise_wa(g):
             nc.vector.quantize_mx(
@@ -256,18 +275,19 @@ def tile_multiheadlatentattention_pa_kernel(tc, x, Wkv_a, kv_norm_w, Wkv_b, out_
 
         def sum_of_squares(a):
             squares = scrap.tile([P, LATENT], BF16, name="squares")
-            nc.scalar.activation(out=squares[:], in_=in_psum["latent", a][:], func=ACT.Square, accum_out=sum_squares[a][:])
+            nc.scalar.activation(out=squares[:], in_=in_psum["latent", a][:], func=ACT.Square, accum_out=sum_squares[:, a : a + 1])
 
-        def find_inv_rms(a):
+        def find_inv_rms(pair):
+            both_tiles = slice(2 * pair, 2 * pair + 2)
             nc.scalar.activation(
-                out=inv_rms[a][:], in_=sum_squares[a][:], func=ACT.Abs_reciprocal_sqrt, scale=1.0 / LATENT, bias=eps[:]
+                out=inv_rms[:, both_tiles], in_=sum_squares[:, both_tiles], func=ACT.Abs_reciprocal_sqrt, scale=1.0 / LATENT, bias=eps[:]
             )
 
         def normalise(a):
             nc.vector.scalar_tensor_tensor(
                 out=normed[a][:],
                 in0=in_psum["latent", a][:],
-                scalar=inv_rms[a][:],
+                scalar=inv_rms[:, a : a + 1],
                 in1=gain[:],
                 op0=ALU.mult,
                 op1=ALU.mult,
@@ -275,18 +295,20 @@ def tile_multiheadlatentattention_pa_kernel(tc, x, Wkv_a, kv_norm_w, Wkv_b, out_
 
         def transpose_n(a):
             words = normed[a][:].bitcast(F32)
-            in_psum["n", a] = banks.tile([P, 2, P], F32, name="turned_n", tag="bank")
+            if a % 2 == 0:
+                in_psum["n", a // 2] = banks.tile([P, 2, 2, P], F32, name="turned_n", tag="bank")
             for u in range(2):
-                nc.tensor.transpose(in_psum["n", a][:, u, :], words[:, u : 2 * P : 2], identity_f32[:])
+                nc.tensor.transpose(in_psum["n", a // 2][:, a % 2, u, :], words[:, u : 2 * P : 2], identity_f32[:])
 
-        def copy_n(a, copy):
-            copy(out=n_grouped[a][:], in_=in_psum["n", a][:].rearrange("p u r -> p r u"))
+        def copy_n(pair, copy):
+            copy(out=n_grouped[:, 2 * pair : 2 * pair + 2, :, :], in_=in_psum["n", pair][:].rearrange("p a u r -> p a r u"))
 
-        def quantise_n(a):
+        def quantise_n(pair):
+            both_tiles = slice(2 * pair, 2 * pair + 2)
             nc.vector.quantize_mx(
-                out=n_codes[a][:].bitcast(FP8X4),
-                scales=n_scales[a][:],
-                in_=n_grouped[a][:].rearrange("p r u -> p (r u)").bitcast(BF16),
+                out=n_codes[:, both_tiles, :].rearrange("p a r -> p (a r)").bitcast(FP8X4),
+                scales=n_scales[:, both_tiles, :].rearrange("p a r -> p (a r)"),
+                in_=n_grouped[:, both_tiles, :, :].rearrange("p a r u -> p (a r u)").bitcast(BF16),
             )
 
         def regroup_wb(j, first, last, copy):
@@ -302,6 +324,14 @@ def tile_multiheadlatentattention_pa_kernel(tc, x, Wkv_a, kv_norm_w, Wkv_b, out_
                 in_=from_heads[:, :, head + first : head + last, kind, :, :].rearrange("p t h c i -> p h c t i"),
             )
 
+        def regroup_wb_half(j):
+            if j not in wb_grouped:
+                wb_grouped[j] = regrouped.tile([P, PIECE_COLS, PACK], BF16, name="wb_grouped", align_bytes=64)
+            chunk, kind = PIECE_ORDER[j]
+            from_heads = wb_raw[chunk][:].rearrange("p t (h k c) -> p t h k c", k=2, c=HEAD_DIM)
+            bank = regroup_by_tensor(lambda h: from_heads[:, :, CHUNK_HEADS // 2 + h, kind, :])
+            nc.scalar.copy(out=wb_grouped[j][:, PIECE_COLS // 2 :, :], in_=bank)
+
         def quantise_wb(j):
             nc.vector.quantize_mx(
                 out=wb_codes[j][:].bitcast(FP8X4),
@@ -313,8 +343,8 @@ def tile_multiheadlatentattention_pa_kernel(tc, x, Wkv_a, kv_norm_w, Wkv_b, out_
             in_psum["kv", a, j] = banks.tile([P, PIECE_COLS], F32, name="kv", tag="bank")
             nc.tensor.matmul_mx(
                 out=in_psum["kv", a, j][:],
-                lhsT=n_codes[a][:].bitcast(FP8X4),
-                lhsT_scale=n_scales[a][:],
+                lhsT=n_codes[:, a, :].bitcast(FP8X4),
+                lhsT_scale=n_scales[:, a, :],
                 rhs=wb_codes[j][:].bitcast(FP8X4),
                 rhs_scale=wb_scales[j][:],
                 start=True,
@@ -371,88 +401,87 @@ def tile_multiheadlatentattention_pa_kernel(tc, x, Wkv_a, kv_norm_w, Wkv_b, out_
         spread_gain(vector)
         regroup_wa(0, 0, LATENT, vector)
         quantise_wa(0)
-        for a in (0, 1):
-            keep_clock(1)
-            for h in range(2):
-                transpose_x(a, h)
-                copy_x(a, h, scalar)
-            regroup_wr(a, scalar)
-        quantise_x(0)
-        regroup_wa(1, 0, LATENT, vector)
-        quantise_x(1)
-        quantise_wa(1)
         keep_clock(1)
+        for h in range(2):
+            transpose_x(0, h)
+            copy_x(0, h, scalar)
+        quantise_x(0)
+        keep_clock(1)
+        for h in range(2):
+            transpose_x(1, h)
+            copy_x(1, h, scalar)
+        regroup_wa(1, 0, half, vector)
+        regroup_wr(0, vector)
+        regroup_wa_half(1)
         for h in range(2):
             transpose_x(2, h)
             copy_x(2, h, scalar)
-        for a in (0, 1):
-            for g in (0, 1):
-                latent_pass(a, g)
+        quantise_wa(1)
+        quantise_x(1)
         regroup_wa(2, 0, half, vector)
-        regroup_wa(2, half, LATENT, scalar)
+        regroup_wa_half(2)
+        for g in (0, 1):
+            latent_pass(0, g)
         quantise_x(2)
-        regroup_wr(2, scalar)
-        quantise_wa(2)
         for h in range(2):
             transpose_x(3, h)
+        for g in (0, 1):
+            latent_pass(1, g)
+        quantise_wa(2)
+        regroup_wa(3, 0, half, vector)
+        regroup_wr(1, vector)
+        regroup_wr(2, vector)
+        regroup_wa(3, half, LATENT, scalar)
+        for h in range(2):
             copy_x(3, h, scalar)
         for g in (0, 1):
             latent_pass(2, g)
         for a in (0, 1, 2):
             latent_pass(a, 2)
-        regroup_wa(3, 0, LATENT, vector)
-        regroup_wr(3, scalar)
         quantise_wa(3)
         for a in (0, 1, 2):
             latent_pass(a, 3)
-        quantise_x(3)
-        for g in range(PASSES):
-            latent_pass(3, g)
         sum_of_squares(0)
         sum_of_squares(1)
         find_inv_rms(0)
-        find_inv_rms(1)
+        regroup_wb(0, 0, CHUNK_HEADS // 2, vector)
+        regroup_wb_half(0)
+        quantise_x(3)
+        regroup_wr(3, vector)
+        for g in range(PASSES):
+            latent_pass(3, g)
+        for a in (0, 1):
+            normalise(a)
+            transpose_n(a)
         sum_of_squares(2)
-        regroup_wb(0, 0, CHUNK_HEADS, vector)
-        normalise(0)
-        transpose_n(0)
-        keep_clock(1)
-        copy_n(0, scalar)
         sum_of_squares(3)
-        find_inv_rms(2)
-        find_inv_rms(3)
+        copy_n(0, scalar)
+        find_inv_rms(1)
         quantise_wb(0)
-        normalise(1)
-        transpose_n(1)
-        keep_clock(1)
-        copy_n(1, scalar)
+        regroup_wb(1, 0, CHUNK_HEADS // 2, vector)
+        regroup_wb_half(1)
         quantise_n(0)
-        product(0, 0)
-        normalise(2)
-        transpose_n(2)
-        keep_clock(1)
-        quantise_n(1)
-        product(1, 0)
-        normalise(3)
-        transpose_n(3)
-        keep_clock(1)
-        copy_n(2, scalar)
-        leave(0, 0, scalar)
-        copy_n(3, scalar)
-        leave(1, 0, scalar)
-        regroup_wb(1, 0, CHUNK_HEADS, vector)
-        quantise_n(2)
-        product(2, 0)
-        quantise_n(3)
-        product(3, 0)
-        leave(2, 0, scalar)
-        leave(3, 0, scalar)
+        for a in (0, 1):
+            product(a, 0)
+        for a in (0, 1):
+            leave(a, 0, scalar)
+        for a in (2, 3):
+            normalise(a)
+            transpose_n(a)
+        copy_n(1, scalar)
         quantise_wb(1)
-        for a in range(TILES):
+        for a in (0, 1):
             product(a, 1)
         regroup_wb(2, 0, CHUNK_HEADS, vector)
-        for a in range(TILES):
+        quantise_n(1)
+        for j in (0, 1):
+            for a in (2, 3):
+                product(a, j)
+        for a in (0, 1):
             leave(a, 1, scalar)
+        for j in (0, 1):
+            for a in (2, 3):
+                leave(a, j, scalar)
         quantise_wb(2)
         regroup_wb(3, 0, CHUNK_HEADS, vector)
         for j in (2, 3):
@@ -461,27 +490,29 @@ def tile_multiheadlatentattention_pa_kernel(tc, x, Wkv_a, kv_norm_w, Wkv_b, out_
             for a in range(TILES):
                 product(a, j)
             for a in range(TILES):
-                leave(a, j, scalar)
-        regroup_wb(6, 0, CHUNK_HEADS, vector)
+                leave(a, j, vector if j == 3 and a == TILES - 1 else scalar)
         quantise_wb(5)
+        regroup_wb(6, 0, CHUNK_HEADS, vector)
         for a in range(TILES):
             for j in (4, 5):
                 product(a, j)
         for a in range(TILES):
             for j in (4, 5):
                 leave(a, j, scalar)
-        quantise_wr()
-        rope_key()
         regroup_wb(7, 0, CHUNK_HEADS, vector)
         quantise_wb(6)
         quantise_wb(7)
-        rope_products()
+        quantise_wr()
         for a in range(TILES):
             for j in (6, 7):
                 product(a, j)
-        rope_sum()
+            if a == 1:
+                rope_key()
         for a in range(TILES):
             for j in (6, 7):
-                leave(a, j, vector if a == TILES - 1 else scalar)
+                leave(a, j, vector if a == 1 else scalar)
+            if a == 1:
+                rope_products()
+                rope_sum()
             if a == TILES - 2:
                 store_rope()

@@ -428,10 +428,8 @@ def tile_multiheadlatentattention_pa_kernel(tc, x, Wkv_a, kv_norm_w, Wkv_b, out_
         for g in (0, 1):
             latent_pass(1, g)
         quantise_wa(2)
-        regroup_wa(3, 0, half, vector)
-        regroup_wr(1, vector)
-        regroup_wr(2, vector)
-        regroup_wa(3, half, LATENT, scalar)
+        regroup_wa(3, 0, 320, vector)
+        regroup_wa(3, 320, LATENT, scalar)
         for h in range(2):
             copy_x(3, h, scalar)
         for g in (0, 1):
@@ -502,6 +500,8 @@ def tile_multiheadlatentattention_pa_kernel(tc, x, Wkv_a, kv_norm_w, Wkv_b, out_
         regroup_wb(7, 0, CHUNK_HEADS, vector)
         quantise_wb(6)
         quantise_wb(7)
+        for g in (1, 2):
+            regroup_wr(g, vector)
         quantise_wr()
         for a in range(TILES):
             for j in (6, 7):
@@ -514,5 +514,4 @@ def tile_multiheadlatentattention_pa_kernel(tc, x, Wkv_a, kv_norm_w, Wkv_b, out_
             if a == 1:
                 rope_products()
                 rope_sum()
-            if a == TILES - 2:
-                store_rope()
+        store_rope()

from contextlib import ExitStack

import concourse.mybir as mybir
from concourse.masks import make_identity

F32 = mybir.dt.float32
BF16 = mybir.dt.bfloat16
I32 = mybir.dt.int32
U32 = mybir.dt.uint32
U8 = mybir.dt.uint8
FP8X4 = mybir.dt.float8_e4m3fn_x4
ALU = mybir.AluOpType
ACT = mybir.ActivationFunctionType

P = 128
PACK = 4
K_PASS = P * PACK
TOKENS = 512
TILES = TOKENS // P
SEQ_HALVES = 2
D_MODEL = 2048
PASSES = D_MODEL // K_PASS
LATENT = 512
ROPE = 128
ROPE_PAIRS = ROPE // 2
A_COLS = LATENT + ROPE
KV_COLS = 4096
HEAD_DIM = 128
CHUNK_COLS = 1024
CHUNK_HEADS = CHUNK_COLS // (2 * HEAD_DIM)
CHUNKS = KV_COLS // CHUNK_COLS
PIECE_COLS = CHUNK_HEADS * HEAD_DIM
PIECES = 2 * CHUNKS
LOAD_COLS = (CHUNK_COLS, CHUNK_COLS, 2 * CHUNK_COLS)
PIECE_ORDER = ((0, 0), (0, 1), (1, 0), (1, 1), (2, 0), (3, 0), (2, 1), (3, 1))
FIRST_PAIRED = 4
RMS_EPS = 1.1920928955078125e-07
ROPE_BASE = 10000.0
TWO_PI = 6.283185307179586

FLOPS = 2 * TOKENS * D_MODEL * A_COLS + 2 * TOKENS * LATENT * KV_COLS

WA_VECTOR_COLS = 256
RUN = 4


def tile_multiheadlatentattention_pa_kernel(tc, x, Wkv_a, kv_norm_w, Wkv_b, out_0, out_1, out_2):
    nc = tc.nc
    x_rows = x.flatten_outer_dims()
    kv_out = [
        out_0.rearrange("b s h d -> (b s) (h d)"),
        out_1.rearrange("b s h d -> (b s) (h d)"),
    ]
    with ExitStack() as ctx:
        keep = ctx.enter_context(tc.tile_pool(name="keep", bufs=1))
        regrouped = ctx.enter_context(tc.tile_pool(name="regrouped", bufs=3))
        scrap = ctx.enter_context(tc.tile_pool(name="scrap", bufs=2))
        leaving = ctx.enter_context(tc.tile_pool(name="leaving", bufs=10))
        leaving_pairs = ctx.enter_context(tc.tile_pool(name="leaving_pairs", bufs=8))
        banks = ctx.enter_context(tc.psum_pool(name="banks", bufs=7))
        idle_bank = ctx.enter_context(tc.psum_pool(name="idle_bank", bufs=1))
        ctx.enter_context(tc.manual_schedule())

        wa_raw = [keep.tile([P, PACK, A_COLS], BF16, name="wa_raw%d" % g) for g in range(PASSES)]
        wa_grouped = [
            keep.tile([P, LATENT, PACK], BF16, name="wa_grouped%d" % g, align_bytes=64) for g in range(PASSES)
        ]
        wa_codes = [keep.tile([P, LATENT], U32, name="wa_codes%d" % g, align_bytes=64) for g in range(PASSES)]
        wa_scales = [keep.tile([P, LATENT], U8, name="wa_scales%d" % g, align_bytes=64) for g in range(PASSES)]
        wr_grouped = keep.tile([P, PASSES, ROPE, PACK], BF16, name="wr_grouped", align_bytes=64)
        wr_codes = keep.tile([P, PASSES, ROPE], U32, name="wr_codes", align_bytes=64)
        wr_scales = keep.tile([P, PASSES, ROPE], U8, name="wr_scales", align_bytes=64)
        x_raw = [keep.tile([P, D_MODEL], BF16, name="x_raw%d" % a) for a in range(TILES)]
        x_grouped = [keep.tile([P, PASSES, P, 2], F32, name="x_grouped%d" % a, align_bytes=64) for a in range(TILES)]
        x_codes = [keep.tile([P, PASSES * P], U32, name="x_codes%d" % a, align_bytes=64) for a in range(TILES)]
        x_scales = [keep.tile([P, PASSES * P], U8, name="x_scales%d" % a, align_bytes=64) for a in range(TILES)]
        sum_squares = keep.tile([P, TILES], F32, name="sum_squares")
        inv_rms = keep.tile([P, TILES], F32, name="inv_rms")
        normed = [keep.tile([P, LATENT], BF16, name="normed%d" % a) for a in range(TILES)]
        n_grouped = keep.tile([P, TILES, P, 2], F32, name="n_grouped", align_bytes=64)
        n_codes = keep.tile([P, TILES, P], U32, name="n_codes", align_bytes=64)
        n_scales = keep.tile([P, TILES, P], U8, name="n_scales", align_bytes=64)
        wb_raw = [keep.tile([P, PACK, LOAD_COLS[c]], BF16, name="wb_raw%d" % c) for c in range(len(LOAD_COLS))]
        wb_codes = [keep.tile([P, PIECE_COLS], U32, name="wb_codes%d" % j, align_bytes=64) for j in range(PIECES)]
        wb_scales = [keep.tile([P, PIECE_COLS], U8, name="wb_scales%d" % j, align_bytes=64) for j in range(PIECES)]
        out_tiles = {}
        in_psum = {}
        wb_grouped = {}

        def load_wa(g):
            nc.sync.dma_start(
                out=wa_raw[g][:],
                in_=Wkv_a[K_PASS * g : K_PASS * (g + 1), :].rearrange("(p t) c -> p t c", t=PACK),
            )

        def load_x(a):
            nc.sync.dma_start(out=x_raw[a][:], in_=x_rows[P * a : P * (a + 1), :])

        def load_wb(c):
            first = sum(LOAD_COLS[:c])
            nc.sync.dma_start(
                out=wb_raw[c][:],
                in_=Wkv_b[:, first : first + LOAD_COLS[c]].rearrange("(p t) n -> p t n", t=PACK),
            )

        gain_row = keep.tile([P, LATENT], BF16, name="gain_row")
        nc.vector.memset(gain_row[:], 0.0)
        position = keep.tile([P, SEQ_HALVES], I32, name="position")
        nc.gpsimd.iota(position[:], pattern=[[P, SEQ_HALVES]], base=0, channel_multiplier=1)
        identity_f32 = keep.tile([P, P], F32, name="identity_f32")
        make_identity(nc, identity_f32[:])
        identity_bf16 = keep.tile([P, P], BF16, name="identity_bf16")
        nc.gpsimd.tensor_copy(out=identity_bf16[:], in_=identity_f32[:])
        ones = keep.tile([P, P], BF16, name="ones")
        nc.vector.memset(ones[:], 1.0)
        zeros = keep.tile([P, LATENT], BF16, name="zeros")
        nc.vector.memset(zeros[:], 0.0)
        eps = keep.tile([P, 1], F32, name="eps")
        nc.vector.memset(eps[:], RMS_EPS)
        table_loaded = keep.tile([P, 2], F32, name="table_loaded")
        nc.scalar.activation(out=table_loaded[:, 0:1], in_=eps[:], func=ACT.Sin)

        load_wa(0)
        nc.sync.dma_start(out=gain_row[0:1, :], in_=kv_norm_w.rearrange("(o n) -> o n", o=1))
        load_x(0)
        load_x(1)
        load_wa(1)
        load_x(2)
        load_wa(2)
        load_x(3)
        load_wa(3)
        load_wb(0)
        load_wb(1)
        load_wb(2)

        turns = keep.tile([P, ROPE_PAIRS, SEQ_HALVES], F32, name="turns")
        nc.vector.tensor_scalar_mul(out=turns[:, 0, :], in0=position[:], scalar1=1.0 / TWO_PI)
        for filled in (1, 4, 16):
            for run in (1, 2, 3):
                nc.vector.tensor_scalar_mul(
                    out=turns[:, run * filled : (run + 1) * filled, :],
                    in0=turns[:, 0:filled, :],
                    scalar1=ROPE_BASE ** (-2.0 * run * filled / ROPE),
                )
        QUARTER = (0.0, 0.25)
        whole = keep.tile([P, 2, SEQ_HALVES, ROPE_PAIRS], I32, name="whole")
        part_turn = keep.tile([P, 2, SEQ_HALVES, ROPE_PAIRS], F32, name="part_turn")
        half_by_half = turns[:].rearrange("p i h -> p h i")
        for s in range(2):
            nc.vector.tensor_scalar_add(out=whole[:, s, :, :], in0=half_by_half, scalar1=QUARTER[s])
        for s in range(2):
            nc.vector.scalar_tensor_tensor(
                out=part_turn[:, s, :, :],
                in0=half_by_half,
                scalar=QUARTER[s],
                in1=whole[:, s, :, :],
                op0=ALU.add,
                op1=ALU.subtract,
            )
        SIN, COS, MINUS_SIN = 0, 1, 2
        trig = keep.tile([P, 3, SEQ_HALVES * ROPE_PAIRS], F32, name="trig")
        for out, angle, sign in ((SIN, SIN, 1.0), (COS, COS, 1.0), (MINUS_SIN, SIN, -1.0)):
            nc.scalar.activation(
                out=trig[:, out, :],
                in_=part_turn[:, angle, :, :].rearrange("p h i -> p (h i)"),
                func=ACT.Sin,
                scale=sign * TWO_PI,
            )
        nc.scalar.activation(out=table_loaded[:, 1:2], in_=eps[:], func=ACT.Abs_reciprocal_sqrt)
        gain = keep.tile([P, LATENT], F32, name="gain")

        def regroup_wa(g, first, last, copy):
            copy(
                out=wa_grouped[g][:, first:last, :].rearrange("p (c i) t -> p c t i", i=RUN),
                in_=wa_raw[g][:, :, first:last].rearrange("p t (c i) -> p c t i", i=RUN),
            )

        def regroup_by_tensor(rows):
            bank = banks.tile([P, 2, HEAD_DIM, PACK], BF16, name="regrouped_rows", tag="bank")
            for h in range(2):
                nc.tensor.matmul(
                    out=bank[:, h, :, :],
                    lhsT=identity_bf16[:],
                    rhs=rows(h).rearrange("p t c -> p c t"),
                    start=True,
                    stop=True,
                )
            return bank[:].rearrange("p h c t -> p (h c) t")

        def regroup_wa_half(g):
            half = LATENT // 2
            bank = regroup_by_tensor(lambda h: wa_raw[g][:, :, half + HEAD_DIM * h : half + HEAD_DIM * (h + 1)])
            nc.scalar.copy(out=wa_grouped[g][:, half:LATENT, :], in_=bank)

        def quantise_wa(g):
            nc.vector.quantize_mx(
                out=wa_codes[g][:].bitcast(FP8X4),
                scales=wa_scales[g][:],
                in_=wa_grouped[g][:].rearrange("p c t -> p (c t)"),
            )

        def regroup_wr(g, copy):
            copy(
                out=wr_grouped[:, g, :, :].rearrange("p (c i) t -> p c t i", i=RUN),
                in_=wa_raw[g][:, :, LATENT:A_COLS].rearrange("p t (c i) -> p c t i", i=RUN),
            )

        def quantise_wr():
            nc.vector.quantize_mx(
                out=wr_codes[:].rearrange("p g c -> p (g c)").bitcast(FP8X4),
                scales=wr_scales[:].rearrange("p g c -> p (g c)"),
                in_=wr_grouped[:].rearrange("p g c t -> p (g c t)"),
            )

        unread = idle_bank.tile([P, LATENT], F32, name="unread")

        def keep_clock(times):
            for repeat in range(times):
                nc.tensor.matmul(out=unread[:], lhsT=ones[:], rhs=zeros[:], start=True, stop=True)

        def spread_gain(copy):
            summed = banks.tile([P, LATENT], F32, name="summed", tag="bank")
            nc.tensor.matmul(out=summed[:], lhsT=ones[:], rhs=gain_row[:], start=True, stop=True)
            copy(out=gain[:], in_=summed[:])

        def transpose_x(a, h):
            words = x_raw[a][:].bitcast(F32)
            in_psum["x", a, h] = banks.tile([P, 2, 2, P], F32, name="turned", tag="bank")
            for g in range(2):
                for u in range(2):
                    first_word = 2 * P * (2 * h + g)
                    nc.tensor.transpose(
                        in_psum["x", a, h][:, g, u, :], words[:, first_word + u : first_word + 2 * P : 2], identity_f32[:]
                    )

        def copy_x(a, h, copy):
            copy(
                out=x_grouped[a][:, 2 * h : 2 * h + 2, :, :],
                in_=in_psum["x", a, h][:].rearrange("p g u r -> p g r u"),
            )

        def quantise_x(a):
            nc.vector.quantize_mx(
                out=x_codes[a][:].bitcast(FP8X4),
                scales=x_scales[a][:],
                in_=x_grouped[a][:].rearrange("p g r u -> p (g r u)").bitcast(BF16),
            )

        def latent_pass(a, g):
            if g == 0:
                in_psum["latent", a] = banks.tile([P, LATENT], F32, name="latent", tag="bank")
            nc.tensor.matmul_mx(
                out=in_psum["latent", a][:],
                lhsT=x_codes[a][:, P * g : P * (g + 1)].bitcast(FP8X4),
                lhsT_scale=x_scales[a][:, P * g : P * (g + 1)],
                rhs=wa_codes[g][:].bitcast(FP8X4),
                rhs_scale=wa_scales[g][:],
                start=(g == 0),
                stop=(g == PASSES - 1),
            )

        def rope_key():
            in_psum["rope"] = banks.tile([P, TILES, ROPE], F32, name="raw_rope", tag="bank")
            for a in range(TILES):
                for g in range(PASSES):
                    nc.tensor.matmul_mx(
                        out=in_psum["rope"][:, a, :],
                        lhsT=x_codes[a][:, P * g : P * (g + 1)].bitcast(FP8X4),
                        lhsT_scale=x_scales[a][:, P * g : P * (g + 1)],
                        rhs=wr_codes[:, g, :].bitcast(FP8X4),
                        rhs_scale=wr_scales[:, g, :],
                        start=(g == 0),
                        stop=(g == PASSES - 1),
                    )

        def sum_of_squares(a):
            squares = scrap.tile([P, LATENT], BF16, name="squares")
            nc.scalar.activation(out=squares[:], in_=in_psum["latent", a][:], func=ACT.Square, accum_out=sum_squares[:, a : a + 1])

        def find_inv_rms(pair):
            both_tiles = slice(2 * pair, 2 * pair + 2)
            nc.scalar.activation(
                out=inv_rms[:, both_tiles], in_=sum_squares[:, both_tiles], func=ACT.Abs_reciprocal_sqrt, scale=1.0 / LATENT, bias=eps[:]
            )

        def normalise(a):
            nc.vector.scalar_tensor_tensor(
                out=normed[a][:],
                in0=in_psum["latent", a][:],
                scalar=inv_rms[:, a : a + 1],
                in1=gain[:],
                op0=ALU.mult,
                op1=ALU.mult,
            )

        def transpose_n(a):
            words = normed[a][:].bitcast(F32)
            if a % 2 == 0:
                in_psum["n", a // 2] = banks.tile([P, 2, 2, P], F32, name="turned_n", tag="bank")
            for u in range(2):
                nc.tensor.transpose(in_psum["n", a // 2][:, a % 2, u, :], words[:, u : 2 * P : 2], identity_f32[:])

        def copy_n(pair, copy):
            copy(out=n_grouped[:, 2 * pair : 2 * pair + 2, :, :], in_=in_psum["n", pair][:].rearrange("p a u r -> p a r u"))

        def quantise_n(pair):
            both_tiles = slice(2 * pair, 2 * pair + 2)
            nc.vector.quantize_mx(
                out=n_codes[:, both_tiles, :].rearrange("p a r -> p (a r)").bitcast(FP8X4),
                scales=n_scales[:, both_tiles, :].rearrange("p a r -> p (a r)"),
                in_=n_grouped[:, both_tiles, :, :].rearrange("p a r u -> p (a r u)").bitcast(BF16),
            )

        def regroup_wb(j, first, last, copy):
            if j not in wb_grouped:
                wb_grouped[j] = regrouped.tile([P, PIECE_COLS, PACK], BF16, name="wb_grouped", align_bytes=64)
            to_heads = wb_grouped[j][:].rearrange("p (h c i) t -> p h c t i", h=CHUNK_HEADS, i=RUN)
            chunk, kind = PIECE_ORDER[j]
            load = min(chunk, len(LOAD_COLS) - 1)
            head = CHUNK_HEADS * (chunk - load)
            from_heads = wb_raw[load][:].rearrange("p t (h k c i) -> p t h k c i", k=2, c=HEAD_DIM // RUN, i=RUN)
            copy(
                out=to_heads[:, first:last],
                in_=from_heads[:, :, head + first : head + last, kind, :, :].rearrange("p t h c i -> p h c t i"),
            )

        def regroup_wb_half(j):
            if j not in wb_grouped:
                wb_grouped[j] = regrouped.tile([P, PIECE_COLS, PACK], BF16, name="wb_grouped", align_bytes=64)
            chunk, kind = PIECE_ORDER[j]
            from_heads = wb_raw[chunk][:].rearrange("p t (h k c) -> p t h k c", k=2, c=HEAD_DIM)
            bank = regroup_by_tensor(lambda h: from_heads[:, :, CHUNK_HEADS // 2 + h, kind, :])
            nc.scalar.copy(out=wb_grouped[j][:, PIECE_COLS // 2 :, :], in_=bank)

        def quantise_wb(j):
            nc.vector.quantize_mx(
                out=wb_codes[j][:].bitcast(FP8X4),
                scales=wb_scales[j][:],
                in_=wb_grouped[j][:].rearrange("p c t -> p (c t)"),
            )

        def product(a, j):
            in_psum["kv", a, j] = banks.tile([P, PIECE_COLS], F32, name="kv", tag="bank")
            nc.tensor.matmul_mx(
                out=in_psum["kv", a, j][:],
                lhsT=n_codes[:, a, :].bitcast(FP8X4),
                lhsT_scale=n_scales[:, a, :],
                rhs=wb_codes[j][:].bitcast(FP8X4),
                rhs_scale=wb_scales[j][:],
                start=True,
                stop=True,
            )

        def leave(a, j, copy):
            chunk, kind = PIECE_ORDER[j]
            pair = j >= FIRST_PAIRED
            if pair and chunk % 2 == 0:
                out_tiles[a] = leaving_pairs.tile([P, 2, PIECE_COLS], F32, name="out_pair")
            elif not pair:
                out_tiles[a] = leaving.tile([P, 1, PIECE_COLS], F32, name="out_tile")
            part = chunk % 2 if pair else 0
            copy(out=out_tiles[a][:, part, :], in_=in_psum["kv", a, j][:])
            if not pair or part == 1:
                nc.sync.dma_start(
                    out=kv_out[kind][P * a : P * (a + 1), PIECE_COLS * (chunk - part) : PIECE_COLS * (chunk + 1)],
                    in_=out_tiles[a][:].rearrange("p s c -> p (s c)"),
                )

        both = [P, 2, P]
        by_cos = keep.tile([P, 2, P, 2], F32, name="by_cos")
        by_sin = keep.tile([P, 2, 2, P], F32, name="by_sin")
        k_rope = keep.tile([P, 2, P, 2], F32, name="k_rope")

        def rope_products():
            pairs = in_psum["rope"][:].rearrange("p (b h) (i e) -> p b (h i) e", b=2, e=2)
            nc.vector.tensor_tensor(
                out=by_cos[:], in0=pairs, in1=trig[:, COS, :].unsqueeze(1).unsqueeze(3).to_broadcast([P, 2, P, 2]), op=ALU.mult
            )
            nc.vector.tensor_tensor(
                out=by_sin[:, 0, :, :], in0=pairs[:, :, :, 1], in1=trig[:, MINUS_SIN, :].unsqueeze(1).to_broadcast(both), op=ALU.mult
            )
            nc.vector.tensor_tensor(
                out=by_sin[:, 1, :, :], in0=pairs[:, :, :, 0], in1=trig[:, SIN, :].unsqueeze(1).to_broadcast(both), op=ALU.mult
            )

        def rope_sum():
            nc.vector.tensor_tensor(
                out=k_rope[:], in0=by_cos[:], in1=by_sin[:].rearrange("p e b n -> p b n e"), op=ALU.add
            )

        def store_rope():
            nc.sync.dma_start(
                out=out_2.rearrange("b (h p) o d -> p (b h) (o d)", h=SEQ_HALVES, p=P),
                in_=k_rope[:].rearrange("p b (h i) e -> p (b h) (i e)", h=SEQ_HALVES),
            )

        vector, scalar = nc.vector.tensor_copy, nc.scalar.copy

        half = LATENT // 2
        keep_clock(4)
        spread_gain(vector)
        regroup_wa(0, 0, LATENT, vector)
        quantise_wa(0)
        keep_clock(1)
        for h in range(2):
            transpose_x(0, h)
            copy_x(0, h, scalar)
        quantise_x(0)
        keep_clock(1)
        for h in range(2):
            transpose_x(1, h)
            copy_x(1, h, scalar)
        regroup_wa(1, 0, half, vector)
        regroup_wr(0, vector)
        regroup_wa_half(1)
        for h in range(2):
            transpose_x(2, h)
            copy_x(2, h, scalar)
        quantise_wa(1)
        quantise_x(1)
        regroup_wa(2, 0, half, vector)
        regroup_wa_half(2)
        for g in (0, 1):
            latent_pass(0, g)
        quantise_x(2)
        for h in range(2):
            transpose_x(3, h)
        for g in (0, 1):
            latent_pass(1, g)
        quantise_wa(2)
        regroup_wa(3, 0, 320, vector)
        regroup_wa(3, 320, LATENT, scalar)
        for h in range(2):
            copy_x(3, h, scalar)
        for g in (0, 1):
            latent_pass(2, g)
        for a in (0, 1, 2):
            latent_pass(a, 2)
        quantise_wa(3)
        for a in (0, 1, 2):
            latent_pass(a, 3)
        sum_of_squares(0)
        sum_of_squares(1)
        find_inv_rms(0)
        regroup_wb(0, 0, CHUNK_HEADS // 2, vector)
        regroup_wb_half(0)
        quantise_x(3)
        regroup_wr(3, vector)
        for g in range(PASSES):
            latent_pass(3, g)
        for a in (0, 1):
            normalise(a)
            transpose_n(a)
        sum_of_squares(2)
        sum_of_squares(3)
        copy_n(0, scalar)
        find_inv_rms(1)
        quantise_wb(0)
        regroup_wb(1, 0, CHUNK_HEADS // 2, vector)
        regroup_wb_half(1)
        quantise_n(0)
        for a in (0, 1):
            product(a, 0)
        for a in (0, 1):
            leave(a, 0, scalar)
        for a in (2, 3):
            normalise(a)
            transpose_n(a)
        copy_n(1, scalar)
        quantise_wb(1)
        for a in (0, 1):
            product(a, 1)
        regroup_wb(2, 0, CHUNK_HEADS, vector)
        quantise_n(1)
        for j in (0, 1):
            for a in (2, 3):
                product(a, j)
        for a in (0, 1):
            leave(a, 1, scalar)
        for j in (0, 1):
            for a in (2, 3):
                leave(a, j, scalar)
        quantise_wb(2)
        regroup_wb(3, 0, CHUNK_HEADS, vector)
        for j in (2, 3):
            regroup_wb(j + 2, 0, CHUNK_HEADS, vector)
            quantise_wb(j + 1)
            for a in range(TILES):
                product(a, j)
            for a in range(TILES):
                leave(a, j, vector if j == 3 and a == TILES - 1 else scalar)
        quantise_wb(5)
        regroup_wb(6, 0, CHUNK_HEADS, vector)
        for a in range(TILES):
            for j in (4, 5):
                product(a, j)
        for a in range(TILES):
            for j in (4, 5):
                leave(a, j, scalar)
        regroup_wb(7, 0, CHUNK_HEADS, vector)
        quantise_wb(6)
        quantise_wb(7)
        for g in (1, 2):
            regroup_wr(g, vector)
        quantise_wr()
        for a in range(TILES):
            for j in (6, 7):
                product(a, j)
            if a == 1:
                rope_key()
        for a in range(TILES):
            for j in (6, 7):
                leave(a, j, vector if a == 1 else scalar)
            if a == 1:
                rope_products()
                rope_sum()
        store_rope()
